import numpy as np
import ml_dtypes


def mxq(x, axis, fmt="e4m3"):
    dtype, down = {"e4m3": (ml_dtypes.float8_e4m3fn, 7), "e5m2": (ml_dtypes.float8_e5m2, 14)}[fmt]
    v = np.moveaxis(np.asarray(x, np.float32).astype(ml_dtypes.bfloat16).astype(np.float64), axis, -1)
    blocks = v.reshape(v.shape[:-1] + (-1, 32))
    amax = np.abs(blocks).max(-1, keepdims=True)
    byte = np.maximum(np.where(amax > 0, np.frexp(amax)[1] - 1 + 127, 0) - down, 1)
    scale = np.exp2(byte - 127.0)
    codes = (blocks / scale).astype(np.float32).astype(dtype).astype(np.float64)
    return np.moveaxis((codes * scale).reshape(v.shape), -1, axis)


WIDE = False


def mx_kscale(k):
    if not WIDE:
        return np.ones(k)
    levels = np.array([10, -10, 5, -5, 0])
    a = np.random.permutation(np.resize(levels, k // 512 * 4)).reshape(k // 512, 4)
    idx = np.arange(k)
    return np.exp2(a[idx // 512, idx % 128 // 32])


BF16 = ml_dtypes.bfloat16


def bf(x):
    return np.asarray(x, np.float32).astype(BF16)


def f64(x):
    return np.asarray(x).astype(np.float64)


B, S, D, H, KV, HD, F = 1, 512, 2048, 16, 8, 128, 5632
REP = H // KV
NQ = H * HD


def setup_inputs():
    t = mx_kscale(KV * HD).reshape(KV, HD)
    to = np.repeat(t, REP, axis=0).reshape(NQ)
    mask = np.where(np.tril(np.ones((S, S), bool)), np.random.standard_normal((S, S)), -1e9)
    sgn = np.where(np.random.standard_normal((KV, HD)) < 0.0, -1.0, 1.0)
    return {"q_rot": bf(np.random.standard_normal((B, S, H, HD))),
            "k_rot": bf(np.random.standard_normal((B, S, KV, HD))),
            "v": bf((0.25 + np.abs(np.random.standard_normal((B, S, KV, HD)))) * sgn * t),
            "mask": bf(mask),
            "wo": bf(np.random.standard_normal((D, NQ)) * 2.0 / np.sqrt(NQ) / to[None, :]),
            "x": bf(np.random.standard_normal((B, S, D)) * np.random.uniform(0.5, 2.0, (B, S, 1)))}


def reference(q_rot, k_rot, v, mask, wo, x):
    q = f64(q_rot).reshape(B, S, KV, REP, HD).transpose(0, 2, 3, 1, 4).reshape(B, KV, REP * S, HD)
    k = f64(k_rot).transpose(0, 2, 3, 1)
    s = (q @ k / np.sqrt(HD)).reshape(B, KV, REP, S, S) + f64(mask)
    e = np.exp(s - s.max(-1, keepdims=True)).reshape(B, KV, REP * S, S)
    o = (mxq(e, 3, "e4m3") @ mxq(f64(v).transpose(0, 2, 1, 3), 2, "e4m3")) / e.sum(-1, keepdims=True)
    o = o.reshape(B, KV, REP, S, HD).transpose(0, 3, 1, 2, 4).reshape(B, S, NQ)
    return f64(x) + (mxq(o, 2, "e4m3") @ mxq(f64(wo), 1, "e4m3").T)

@@ -1,0 +1,240 @@
+import math
+from contextlib import ExitStack
+
+import concourse.mybir as mybir
+from concourse.masks import make_identity
+
+BF16 = mybir.dt.bfloat16
+F32 = mybir.dt.float32
+U32 = mybir.dt.uint32
+U8 = mybir.dt.uint8
+FP8X4 = mybir.dt.float8_e4m3fn_x4
+ALU = mybir.AluOpType
+ACT = mybir.ActivationFunctionType
+
+P = 128
+S = 512
+H = 16
+KV = 8
+HD = 128
+D = 2048
+NQ = H * HD
+TILES = S // P
+GROUP = 4
+GROUPS = H // GROUP
+BANK = 512
+E_TILES = 2 * GROUP
+SCALE = 1.0 / math.sqrt(HD)
+
+FLOPS = 2 * (2 * H * S * S * HD) + 2 * S * D * NQ
+
+
+def tile_transformerblock_pb_kernel(tc, q_rot, k_rot, v, mask, wo, x, out):
+    nc = tc.nc
+    q2 = q_rot.rearrange("b s h d -> (b s) (h d)")
+    k2 = k_rot.rearrange("b s h d -> (b s) (h d)")
+    v2 = v.rearrange("b s h d -> (b s) (h d)")
+    x2 = x.rearrange("b s d -> (b s) d")
+    out2 = out.rearrange("b s d -> (b s) d")
+
+    with ExitStack() as pools:
+        fixed = pools.enter_context(tc.tile_pool(name="fixed", bufs=1))
+        work = pools.enter_context(tc.tile_pool(name="work", bufs=2))
+        ps_scores = pools.enter_context(tc.psum_pool(name="ps_scores", bufs=2))
+        ps_flip = pools.enter_context(tc.psum_pool(name="ps_flip", bufs=3))
+        ps_heads = pools.enter_context(tc.psum_pool(name="ps_heads", bufs=1))
+        ps_out = pools.enter_context(tc.psum_pool(name="ps_out", bufs=2))
+
+        k_raw = []
+        q_raw = []
+        mask_sb = fixed.tile([P, TILES, S], BF16)
+        v_raw = fixed.tile([P, 2, 2, KV * HD], BF16)
+        for j in range(TILES):
+            k_tile = fixed.tile([P, KV * HD], BF16, name="k_raw%d" % j)
+            nc.sync.dma_start(out=k_tile[:], in_=k2[j * P : (j + 1) * P, :])
+            k_raw.append(k_tile)
+            q_tile = fixed.tile([P, NQ], BF16, name="q_raw%d" % j)
+            nc.sync.dma_start(out=q_tile[:], in_=q2[j * P : (j + 1) * P, :])
+            q_raw.append(q_tile)
+            if j == 0:
+                nc.sync.dma_start(out=mask_sb[:], in_=mask.rearrange("(i p) k -> p i k", p=P))
+            if j == 1:
+                nc.sync.dma_start(out=v_raw[:], in_=v2.rearrange("(u p e) c -> p u e c", u=2, e=2))
+
+        ident_bf = fixed.tile([P, P], BF16)
+        make_identity(nc, ident_bf[:])
+        ident_f32 = fixed.tile([P, P], F32)
+        make_identity(nc, ident_f32[:])
+        e_tiles = []
+        for n in range(E_TILES):
+            e_tile = fixed.tile([P, S], BF16, name="e%d" % n)
+            nc.vector.memset(e_tile[:], 0.0)
+            e_tiles.append(e_tile)
+        negmax = fixed.tile([P, TILES * H], F32)
+        rowsum = fixed.tile([P, TILES * H], F32)
+        rinv = fixed.tile([P, TILES * H], F32)
+
+        kT = fixed.tile([P, KV, S], BF16)
+        qT = fixed.tile([P, H, S], BF16)
+        banks = 0
+        for j in range(TILES):
+            for raw, flipped, n_heads in ((k_raw[j], kT, KV), (q_raw[j], qT, H)):
+                for h0 in range(0, n_heads, 4):
+                    flip = ps_flip.tile([P, 4, P], BF16, tag="flip")
+                    for c in range(4):
+                        nc.tensor.transpose(flip[:, c, :], raw[:, (h0 + c) * HD : (h0 + c + 1) * HD], ident_bf[:])
+                    dst = flipped[:, h0 : h0 + 4, j * P : (j + 1) * P]
+                    if banks % 2 == 0:
+                        nc.scalar.copy(out=dst, in_=flip[:])
+                    else:
+                        nc.vector.tensor_copy(out=dst, in_=flip[:])
+                    banks += 1
+
+        v_grouped = fixed.tile([P, KV * HD, 4], BF16, align_bytes=64)
+        nc.vector.tensor_copy(out=v_grouped[:], in_=v_raw[:].rearrange("p u e c -> p c (u e)"))
+        v_codes = fixed.tile([P, KV * HD], U32, align_bytes=64)
+        v_scales = fixed.tile([P, KV * HD], U8, align_bytes=64)
+        nc.vector.quantize_mx(
+            out=v_codes[:].bitcast(FP8X4), scales=v_scales[:], in_=v_grouped[:].rearrange("p c t -> p (c t)")
+        )
+
+        wo_codes = fixed.tile([P, GROUPS, D], U32, align_bytes=64)
+        wo_scales = fixed.tile([P, GROUPS, D], U8, align_bytes=64)
+        for pr in range(D // (2 * P)):
+            wo_raw = work.tile([P, 2, NQ], BF16, bufs=4)
+            nc.sync.dma_start(
+                out=wo_raw[:], in_=wo[pr * 2 * P : (pr + 1) * 2 * P, :].rearrange("(r p) k -> p r k", p=P)
+            )
+            for g in range(GROUPS):
+                flip = ps_flip.tile([P, 4, P], F32, tag="flip")
+                for r in range(2):
+                    words = wo_raw[:, r, :].bitcast(F32)
+                    for u in range(2):
+                        w0 = 256 * g + 128 * u
+                        nc.tensor.transpose(flip[:, 2 * r + u, :], words[:, w0 : w0 + P], ident_f32[:])
+                wo_grouped = work.tile([P, 4 * 2 * P], BF16, align_bytes=64, bufs=3)
+                nc.scalar.copy(
+                    out=wo_grouped[:].bitcast(F32).rearrange("p (r d u) -> p r d u", r=2, u=2),
+                    in_=flip[:].rearrange("p (r u) d -> p r d u", u=2),
+                )
+                cols = slice(pr * 2 * P, (pr + 1) * 2 * P)
+                nc.vector.quantize_mx(
+                    out=wo_codes[:, g, cols].bitcast(FP8X4), scales=wo_scales[:, g, cols], in_=wo_grouped[:]
+                )
+
+        x_sb = fixed.tile([P, TILES, D], BF16)
+        nc.sync.dma_start(out=x_sb[:], in_=x2.rearrange("(i p) d -> p i d", p=P))
+
+        o_codes = fixed.tile([P, GROUPS, S], U32, align_bytes=64)
+        o_scales = fixed.tile([P, GROUPS, S], U8, align_bytes=64)
+        units = 0
+        for i in range(TILES):
+            rows = slice(i * P, (i + 1) * P)
+            keys = (i + 1) * P
+            per_bank = BANK // keys
+            for g in range(GROUPS):
+                col0 = i * H + g * GROUP
+                group_e = []
+                for h0 in range(g * GROUP, (g + 1) * GROUP, per_bank):
+                    scores = ps_scores.tile([P, BANK], F32)
+                    for a in range(per_bank):
+                        nc.tensor.matmul(
+                            scores[:, a * keys : (a + 1) * keys],
+                            lhsT=qT[:, h0 + a, rows],
+                            rhs=kT[:, (h0 + a) // 2, 0:keys],
+                            start=True,
+                            stop=True,
+                        )
+                    masked = work.tile([P, BANK], F32, bufs=3)
+                    span = per_bank * keys
+                    nc.vector.scalar_tensor_tensor(
+                        out=masked[:, 0:span].rearrange("p (a n) -> p a n", a=per_bank),
+                        in0=scores[:, 0:span].rearrange("p (a n) -> p a n", a=per_bank),
+                        scalar=SCALE,
+                        in1=mask_sb[:, i, 0:keys].unsqueeze(1).to_broadcast([P, per_bank, keys]),
+                        op0=ALU.mult,
+                        op1=ALU.add,
+                    )
+                    c0 = i * H + h0
+                    nc.vector.tensor_reduce(
+                        out=negmax[:, c0 : c0 + per_bank],
+                        in_=masked[:, 0:span].rearrange("p (a n) -> p a n", a=per_bank),
+                        axis=mybir.AxisListType.X,
+                        op=ALU.max,
+                        negate=True,
+                    )
+                    for a in range(per_bank):
+                        e_tile = e_tiles[units % E_TILES]
+                        units += 1
+                        nc.scalar.activation(
+                            out=e_tile[:, 0:keys],
+                            in_=masked[:, a * keys : (a + 1) * keys],
+                            func=ACT.Exp,
+                            bias=negmax[:, c0 + a : c0 + a + 1],
+                            scale=1.0,
+                            accum_out=rowsum[:, c0 + a : c0 + a + 1],
+                        )
+                        group_e.append(e_tile)
+
+                e_grouped = work.tile([P, GROUP * P * 4], BF16, align_bytes=64)
+                e_words = e_grouped[:].bitcast(F32).rearrange("p (a q u) -> p a q u", a=GROUP, u=2)
+                for a0 in range(0, GROUP, 2):
+                    flip = ps_flip.tile([P, 4, P], F32, tag="flip")
+                    for a in range(2):
+                        words = group_e[a0 + a][:].bitcast(F32)
+                        for u in range(2):
+                            nc.tensor.transpose(flip[:, 2 * a + u, :], words[:, u * P : (u + 1) * P], ident_f32[:])
+                    nc.scalar.copy(out=e_words[:, a0 : a0 + 2], in_=flip[:].rearrange("p (a u) q -> p a q u", u=2))
+                e_codes = work.tile([P, GROUP * P], U32, align_bytes=64)
+                e_scales = work.tile([P, GROUP * P], U8, align_bytes=64)
+                nc.vector.quantize_mx(out=e_codes[:].bitcast(FP8X4), scales=e_scales[:], in_=e_grouped[:])
+
+                heads = ps_heads.tile([P, GROUP, HD], F32)
+                for a in range(GROUP):
+                    kv = (g * GROUP + a) // 2
+                    nc.tensor.matmul_mx(
+                        out=heads[:, a, :],
+                        lhsT=e_codes[:, a * P : (a + 1) * P].bitcast(FP8X4),
+                        lhsT_scale=e_scales[:, a * P : (a + 1) * P],
+                        rhs=v_codes[:, kv * HD : (kv + 1) * HD].bitcast(FP8X4),
+                        rhs_scale=v_scales[:, kv * HD : (kv + 1) * HD],
+                        start=True,
+                        stop=True,
+                    )
+                nc.vector.reciprocal(out=rinv[:, col0 : col0 + GROUP], in_=rowsum[:, col0 : col0 + GROUP])
+                o_sb = work.tile([P, GROUP * HD], BF16)
+                for a in range(GROUP):
+                    nc.scalar.activation(
+                        out=o_sb[:, a * HD : (a + 1) * HD],
+                        in_=heads[:, a, :],
+                        func=ACT.Copy,
+                        scale=rinv[:, col0 + a : col0 + a + 1],
+                    )
+                flip = ps_flip.tile([P, 4, P], F32, tag="flip")
+                for u in range(2):
+                    nc.tensor.transpose(flip[:, u, :], o_sb[:].bitcast(F32)[:, u * P : (u + 1) * P], ident_f32[:])
+                o_grouped = work.tile([P, P * 4], BF16, align_bytes=64)
+                nc.scalar.copy(
+                    out=o_grouped[:].bitcast(F32).rearrange("p (q u) -> p q u", u=2),
+                    in_=flip[:, 0:2, :].rearrange("p u q -> p q u"),
+                )
+                nc.vector.quantize_mx(
+                    out=o_codes[:, g, rows].bitcast(FP8X4), scales=o_scales[:, g, rows], in_=o_grouped[:]
+                )
+
+            for n in range(D // BANK):
+                cols = slice(n * BANK, (n + 1) * BANK)
+                acc = ps_out.tile([P, BANK], F32)
+                for g in range(GROUPS):
+                    nc.tensor.matmul_mx(
+                        out=acc[:],
+                        lhsT=o_codes[:, g, rows].bitcast(FP8X4),
+                        lhsT_scale=o_scales[:, g, rows],
+                        rhs=wo_codes[:, g, cols].bitcast(FP8X4),
+                        rhs_scale=wo_scales[:, g, cols],
+                        start=(g == 0),
+                        stop=(g == GROUPS - 1),
+                    )
+                result = work.tile([P, BANK], F32, bufs=4)
+                nc.vector.tensor_tensor(out=result[:], in0=acc[:], in1=x_sb[:, i, cols], op=ALU.add)
+                nc.sync.dma_start(out=out2[rows, cols], in_=result[:])

@@ -23,8 +23,23 @@ TILES = S // P
 GROUP = 4
 GROUPS = H // GROUP
 BANK = 512
+BLOCKS = D // BANK
 E_TILES = 2 * GROUP
 SCALE = 1.0 / math.sqrt(HD)
+
+ROUNDS = TILES * GROUPS
+STEPS = ROUNDS * GROUP
+WO_PAIRS = D // (2 * P)
+WO_ITEMS = WO_PAIRS * GROUPS
+WO_BUFS = 4
+TILE_ORDER = (0, 3, 2, 1)
+FLIP_STEP = 0
+V_STEP = 5
+WO_STEP = 7
+AHEAD = 2
+RESIDUAL_LAG = 2
+WO_QUANT_LAG = 3
+PROJECT_EVERY = 2
 
 FLOPS = 2 * (2 * H * S * S * HD) + 2 * S * D * NQ
 
@@ -37,204 +52,374 @@ def tile_transformerblock_pb_kernel(tc, q_rot, k_rot, v, mask, wo, x, out):
     x2 = x.rearrange("b s d -> (b s) d")
     out2 = out.rearrange("b s d -> (b s) d")
 
-    with ExitStack() as pools:
-        fixed = pools.enter_context(tc.tile_pool(name="fixed", bufs=1))
-        work = pools.enter_context(tc.tile_pool(name="work", bufs=2))
-        ps_scores = pools.enter_context(tc.psum_pool(name="ps_scores", bufs=2))
-        ps_flip = pools.enter_context(tc.psum_pool(name="ps_flip", bufs=3))
-        ps_heads = pools.enter_context(tc.psum_pool(name="ps_heads", bufs=1))
-        ps_out = pools.enter_context(tc.psum_pool(name="ps_out", bufs=2))
+    with ExitStack() as stack:
+        fixed = stack.enter_context(tc.tile_pool(name="fixed", bufs=1))
+        work = stack.enter_context(tc.tile_pool(name="work", bufs=2))
+        ps_scores = stack.enter_context(tc.psum_pool(name="ps_scores", bufs=AHEAD))
+        ps_flip = stack.enter_context(tc.psum_pool(name="ps_flip", bufs=3))
+        ps_side = stack.enter_context(tc.psum_pool(name="ps_side", bufs=2))
+        ps_heads = stack.enter_context(tc.psum_pool(name="ps_heads", bufs=1))
+        stack.enter_context(tc.manual_schedule())
 
-        k_raw = []
-        q_raw = []
-        mask_sb = fixed.tile([P, TILES, S], BF16)
+        def tile_of_round(r):
+            return TILE_ORDER[r // GROUPS]
+
+        def keys_of(i):
+            return (i + 1) * P
+
+        k_raw = [fixed.tile([P, KV * HD], BF16, name="k_raw%d" % j) for j in range(TILES)]
+        q_raw = [fixed.tile([P, NQ], BF16, name="q_raw%d" % i) for i in range(TILES)]
+        mask_sb = [fixed.tile([P, S], BF16, name="mask%d" % i) for i in range(TILES)]
         v_raw = fixed.tile([P, 2, 2, KV * HD], BF16)
-        for j in range(TILES):
-            k_tile = fixed.tile([P, KV * HD], BF16, name="k_raw%d" % j)
-            nc.sync.dma_start(out=k_tile[:], in_=k2[j * P : (j + 1) * P, :])
-            k_raw.append(k_tile)
-            q_tile = fixed.tile([P, NQ], BF16, name="q_raw%d" % j)
-            nc.sync.dma_start(out=q_tile[:], in_=q2[j * P : (j + 1) * P, :])
-            q_raw.append(q_tile)
-            if j == 0:
-                nc.sync.dma_start(out=mask_sb[:], in_=mask.rearrange("(i p) k -> p i k", p=P))
-            if j == 1:
-                nc.sync.dma_start(out=v_raw[:], in_=v2.rearrange("(u p e) c -> p u e c", u=2, e=2))
-
+        x_sb = fixed.tile([P, TILES, D], BF16)
         ident_bf = fixed.tile([P, P], BF16)
-        make_identity(nc, ident_bf[:])
         ident_f32 = fixed.tile([P, P], F32)
-        make_identity(nc, ident_f32[:])
-        e_tiles = []
-        for n in range(E_TILES):
-            e_tile = fixed.tile([P, S], BF16, name="e%d" % n)
-            nc.vector.memset(e_tile[:], 0.0)
-            e_tiles.append(e_tile)
-        negmax = fixed.tile([P, TILES * H], F32)
-        rowsum = fixed.tile([P, TILES * H], F32)
-        rinv = fixed.tile([P, TILES * H], F32)
-
         kT = fixed.tile([P, KV, S], BF16)
         qT = fixed.tile([P, H, S], BF16)
-        banks = 0
-        for j in range(TILES):
-            for raw, flipped, n_heads in ((k_raw[j], kT, KV), (q_raw[j], qT, H)):
-                for h0 in range(0, n_heads, 4):
-                    flip = ps_flip.tile([P, 4, P], BF16, tag="flip")
-                    for c in range(4):
-                        nc.tensor.transpose(flip[:, c, :], raw[:, (h0 + c) * HD : (h0 + c + 1) * HD], ident_bf[:])
-                    dst = flipped[:, h0 : h0 + 4, j * P : (j + 1) * P]
-                    if banks % 2 == 0:
-                        nc.scalar.copy(out=dst, in_=flip[:])
-                    else:
-                        nc.vector.tensor_copy(out=dst, in_=flip[:])
-                    banks += 1
-
+        e_tiles = [fixed.tile([P, S], BF16, name="e%d" % n) for n in range(E_TILES)]
+        e_filled = [S] * E_TILES
+        negmax = fixed.tile([P, STEPS], F32)
+        rowsum = fixed.tile([P, STEPS], F32)
+        rinv = fixed.tile([P, STEPS], F32)
         v_grouped = fixed.tile([P, KV * HD, 4], BF16, align_bytes=64)
-        nc.vector.tensor_copy(out=v_grouped[:], in_=v_raw[:].rearrange("p u e c -> p c (u e)"))
         v_codes = fixed.tile([P, KV * HD], U32, align_bytes=64)
         v_scales = fixed.tile([P, KV * HD], U8, align_bytes=64)
-        nc.vector.quantize_mx(
-            out=v_codes[:].bitcast(FP8X4), scales=v_scales[:], in_=v_grouped[:].rearrange("p c t -> p (c t)")
-        )
-
         wo_codes = fixed.tile([P, GROUPS, D], U32, align_bytes=64)
         wo_scales = fixed.tile([P, GROUPS, D], U8, align_bytes=64)
-        for pr in range(D // (2 * P)):
-            wo_raw = work.tile([P, 2, NQ], BF16, bufs=4)
-            nc.sync.dma_start(
-                out=wo_raw[:], in_=wo[pr * 2 * P : (pr + 1) * 2 * P, :].rearrange("(r p) k -> p r k", p=P)
-            )
-            for g in range(GROUPS):
-                flip = ps_flip.tile([P, 4, P], F32, tag="flip")
-                for r in range(2):
-                    words = wo_raw[:, r, :].bitcast(F32)
-                    for u in range(2):
-                        w0 = 256 * g + 128 * u
-                        nc.tensor.transpose(flip[:, 2 * r + u, :], words[:, w0 : w0 + P], ident_f32[:])
-                wo_grouped = work.tile([P, 4 * 2 * P], BF16, align_bytes=64, bufs=3)
-                nc.scalar.copy(
-                    out=wo_grouped[:].bitcast(F32).rearrange("p (r d u) -> p r d u", r=2, u=2),
-                    in_=flip[:].rearrange("p (r u) d -> p r d u", u=2),
-                )
-                cols = slice(pr * 2 * P, (pr + 1) * 2 * P)
-                nc.vector.quantize_mx(
-                    out=wo_codes[:, g, cols].bitcast(FP8X4), scales=wo_scales[:, g, cols], in_=wo_grouped[:]
-                )
-
-        x_sb = fixed.tile([P, TILES, D], BF16)
-        nc.sync.dma_start(out=x_sb[:], in_=x2.rearrange("(i p) d -> p i d", p=P))
-
         o_codes = fixed.tile([P, GROUPS, S], U32, align_bytes=64)
         o_scales = fixed.tile([P, GROUPS, S], U8, align_bytes=64)
-        units = 0
-        for i in range(TILES):
-            rows = slice(i * P, (i + 1) * P)
-            keys = (i + 1) * P
-            per_bank = BANK // keys
-            for g in range(GROUPS):
-                col0 = i * H + g * GROUP
-                group_e = []
-                for h0 in range(g * GROUP, (g + 1) * GROUP, per_bank):
-                    scores = ps_scores.tile([P, BANK], F32)
-                    for a in range(per_bank):
-                        nc.tensor.matmul(
-                            scores[:, a * keys : (a + 1) * keys],
-                            lhsT=qT[:, h0 + a, rows],
-                            rhs=kT[:, (h0 + a) // 2, 0:keys],
-                            start=True,
-                            stop=True,
-                        )
-                    masked = work.tile([P, BANK], F32, bufs=3)
-                    span = per_bank * keys
-                    nc.vector.scalar_tensor_tensor(
-                        out=masked[:, 0:span].rearrange("p (a n) -> p a n", a=per_bank),
-                        in0=scores[:, 0:span].rearrange("p (a n) -> p a n", a=per_bank),
-                        scalar=SCALE,
-                        in1=mask_sb[:, i, 0:keys].unsqueeze(1).to_broadcast([P, per_bank, keys]),
-                        op0=ALU.mult,
-                        op1=ALU.add,
-                    )
-                    c0 = i * H + h0
-                    nc.vector.tensor_reduce(
-                        out=negmax[:, c0 : c0 + per_bank],
-                        in_=masked[:, 0:span].rearrange("p (a n) -> p a n", a=per_bank),
-                        axis=mybir.AxisListType.X,
-                        op=ALU.max,
-                        negate=True,
-                    )
-                    for a in range(per_bank):
-                        e_tile = e_tiles[units % E_TILES]
-                        units += 1
-                        nc.scalar.activation(
-                            out=e_tile[:, 0:keys],
-                            in_=masked[:, a * keys : (a + 1) * keys],
-                            func=ACT.Exp,
-                            bias=negmax[:, c0 + a : c0 + a + 1],
-                            scale=1.0,
-                            accum_out=rowsum[:, c0 + a : c0 + a + 1],
-                        )
-                        group_e.append(e_tile)
 
-                e_grouped = work.tile([P, GROUP * P * 4], BF16, align_bytes=64)
-                e_words = e_grouped[:].bitcast(F32).rearrange("p (a q u) -> p a q u", a=GROUP, u=2)
-                for a0 in range(0, GROUP, 2):
-                    flip = ps_flip.tile([P, 4, P], F32, tag="flip")
-                    for a in range(2):
-                        words = group_e[a0 + a][:].bitcast(F32)
-                        for u in range(2):
-                            nc.tensor.transpose(flip[:, 2 * a + u, :], words[:, u * P : (u + 1) * P], ident_f32[:])
-                    nc.scalar.copy(out=e_words[:, a0 : a0 + 2], in_=flip[:].rearrange("p (a u) q -> p a q u", u=2))
-                e_codes = work.tile([P, GROUP * P], U32, align_bytes=64)
-                e_scales = work.tile([P, GROUP * P], U8, align_bytes=64)
-                nc.vector.quantize_mx(out=e_codes[:].bitcast(FP8X4), scales=e_scales[:], in_=e_grouped[:])
+        wo_raw = {}
 
-                heads = ps_heads.tile([P, GROUP, HD], F32)
-                for a in range(GROUP):
-                    kv = (g * GROUP + a) // 2
-                    nc.tensor.matmul_mx(
-                        out=heads[:, a, :],
-                        lhsT=e_codes[:, a * P : (a + 1) * P].bitcast(FP8X4),
-                        lhsT_scale=e_scales[:, a * P : (a + 1) * P],
-                        rhs=v_codes[:, kv * HD : (kv + 1) * HD].bitcast(FP8X4),
-                        rhs_scale=v_scales[:, kv * HD : (kv + 1) * HD],
-                        start=True,
-                        stop=True,
-                    )
-                nc.vector.reciprocal(out=rinv[:, col0 : col0 + GROUP], in_=rowsum[:, col0 : col0 + GROUP])
-                o_sb = work.tile([P, GROUP * HD], BF16)
-                for a in range(GROUP):
-                    nc.scalar.activation(
-                        out=o_sb[:, a * HD : (a + 1) * HD],
-                        in_=heads[:, a, :],
-                        func=ACT.Copy,
-                        scale=rinv[:, col0 + a : col0 + a + 1],
-                    )
-                flip = ps_flip.tile([P, 4, P], F32, tag="flip")
+        def load_wo(pr):
+            wo_raw[pr] = work.tile([P, 2, NQ], BF16, name="wo_raw", bufs=WO_BUFS)
+            nc.sync.dma_start(
+                out=wo_raw[pr][:], in_=wo[pr * 2 * P : (pr + 1) * 2 * P, :].rearrange("(r p) k -> p r k", p=P)
+            )
+
+        def load_rows(dst, src, i):
+            nc.sync.dma_start(out=dst[i][:], in_=src[i * P : (i + 1) * P, :])
+
+        first = TILE_ORDER[0]
+        for j in range(first + 1):
+            load_rows(k_raw, k2, j)
+        load_rows(mask_sb, mask, first)
+        load_rows(q_raw, q2, first)
+        for j in range(first + 1, TILES):
+            load_rows(k_raw, k2, j)
+        load_rows(mask_sb, mask, TILE_ORDER[1])
+        load_rows(q_raw, q2, TILE_ORDER[1])
+        nc.sync.dma_start(out=v_raw[:], in_=v2.rearrange("(u p e) c -> p u e c", u=2, e=2))
+        load_wo(0)
+        load_wo(1)
+        for i in TILE_ORDER[2:]:
+            load_rows(mask_sb, mask, i)
+            load_rows(q_raw, q2, i)
+        load_wo(2)
+        load_wo(3)
+        nc.sync.dma_start(out=x_sb[:], in_=x2.rearrange("(i p) d -> p i d", p=P))
+
+        make_identity(nc, ident_bf[:])
+        make_identity(nc, ident_f32[:])
+
+        def flip_heads(raw, h0):
+            flip = ps_flip.tile([P, 4, P], BF16, name="flip")
+            for c in range(4):
+                nc.tensor.transpose(flip[:, c, :], raw[:, (h0 + c) * HD : (h0 + c + 1) * HD], ident_bf[:])
+            return flip
+
+        def k_jobs(j):
+            return [(k_raw[j], h0, kT[:, h0 : h0 + 4, j * P : (j + 1) * P]) for h0 in range(0, KV, 4)]
+
+        def q_jobs(i):
+            return [(q_raw[i], h0, qT[:, h0 : h0 + 4, i * P : (i + 1) * P]) for h0 in range(0, H, 4)]
+
+        head_jobs = []
+        loop_jobs = []
+        for j in range(TILES):
+            (head_jobs if j <= first else loop_jobs).extend(k_jobs(j))
+        head_jobs.extend(q_jobs(first))
+        for i in TILE_ORDER[1:]:
+            loop_jobs.extend(q_jobs(i))
+        for n, (raw, h0, dst) in enumerate(head_jobs):
+            flip = flip_heads(raw, h0)
+            if n % 2 == 0:
+                nc.scalar.copy(out=dst, in_=flip[:])
+            else:
+                nc.vector.tensor_copy(out=dst, in_=flip[:])
+
+        banks = []
+        bank_at_step = {}
+        for r in range(ROUNDS):
+            i = tile_of_round(r)
+            per_bank = BANK // keys_of(i)
+            for a in range(0, GROUP, per_bank):
+                bank_at_step[r * GROUP + a] = len(banks)
+                banks.append((i, (r % GROUPS) * GROUP + a, per_bank))
+        score_tiles = {}
+        masked_banks = {}
+        masked_tiles = {}
+
+        def issue_scores(b):
+            i, h0, per_bank = banks[b]
+            keys = keys_of(i)
+            scores = ps_scores.tile([P, BANK], F32, name="scores")
+            for a in range(per_bank):
+                nc.tensor.matmul(
+                    scores[:, a * keys : (a + 1) * keys],
+                    lhsT=qT[:, h0 + a, i * P : (i + 1) * P],
+                    rhs=kT[:, (h0 + a) // 2, 0:keys],
+                    start=True,
+                    stop=True,
+                )
+            score_tiles[b] = scores
+
+        def add_mask(step):
+            b = bank_at_step[step]
+            i, h0, per_bank = banks[b]
+            keys = keys_of(i)
+            span = per_bank * keys
+            masked = work.tile([P, BANK], F32, name="masked", bufs=4)
+            nc.vector.scalar_tensor_tensor(
+                out=masked[:, 0:span].rearrange("p (a n) -> p a n", a=per_bank),
+                in0=score_tiles[b][:, 0:span].rearrange("p (a n) -> p a n", a=per_bank),
+                scalar=SCALE,
+                in1=mask_sb[i][:, 0:keys].unsqueeze(1).to_broadcast([P, per_bank, keys]),
+                op0=ALU.mult,
+                op1=ALU.add,
+            )
+            masked_banks[step] = masked
+            for a in range(per_bank):
+                masked_tiles[step + a] = masked[:, a * keys : (a + 1) * keys]
+
+        def row_max(step):
+            i, h0, per_bank = banks[bank_at_step[step]]
+            span = per_bank * keys_of(i)
+            nc.vector.tensor_reduce(
+                out=negmax[:, step : step + per_bank],
+                in_=masked_banks[step][:, 0:span].rearrange("p (a n) -> p a n", a=per_bank),
+                axis=mybir.AxisListType.X,
+                op=ALU.max,
+                negate=True,
+            )
+
+        def exponentials(step):
+            keys = keys_of(tile_of_round(step // GROUP))
+            n = step % E_TILES
+            if keys < e_filled[n]:
+                nc.gpsimd.memset(e_tiles[n][:, keys : e_filled[n]], 0.0)
+            e_filled[n] = keys
+            nc.scalar.activation(
+                out=e_tiles[n][:, 0:keys],
+                in_=masked_tiles[step],
+                func=ACT.Exp,
+                bias=negmax[:, step : step + 1],
+                scale=1.0,
+                accum_out=rowsum[:, step : step + 1],
+            )
+
+        e_flips = {}
+        e_grouped = {}
+        e_codes = {}
+        e_scales = {}
+        head_sums = {}
+        o_rows = {}
+        o_flips = {}
+        o_grouped = {}
+
+        def flip_e(r, half):
+            flip = ps_flip.tile([P, 4, P], F32, name="flip")
+            for a in range(2):
+                words = e_tiles[(r * GROUP + 2 * half + a) % E_TILES][:].bitcast(F32)
                 for u in range(2):
-                    nc.tensor.transpose(flip[:, u, :], o_sb[:].bitcast(F32)[:, u * P : (u + 1) * P], ident_f32[:])
-                o_grouped = work.tile([P, P * 4], BF16, align_bytes=64)
-                nc.scalar.copy(
-                    out=o_grouped[:].bitcast(F32).rearrange("p (q u) -> p q u", u=2),
-                    in_=flip[:, 0:2, :].rearrange("p u q -> p q u"),
-                )
-                nc.vector.quantize_mx(
-                    out=o_codes[:, g, rows].bitcast(FP8X4), scales=o_scales[:, g, rows], in_=o_grouped[:]
+                    nc.tensor.transpose(flip[:, 2 * a + u, :], words[:, u * P : (u + 1) * P], ident_f32[:])
+            e_flips[(r, half)] = flip
+
+        def gather_e(r, half):
+            if half == 0:
+                e_grouped[r] = work.tile([P, GROUP * P * 4], BF16, name="e_grouped", align_bytes=64)
+            e_words = e_grouped[r][:].bitcast(F32).rearrange("p (a q u) -> p a q u", a=GROUP, u=2)
+            nc.scalar.copy(
+                out=e_words[:, 2 * half : 2 * half + 2],
+                in_=e_flips[(r, half)][:].rearrange("p (a u) q -> p a q u", u=2),
+            )
+
+        def quantise_e(r):
+            e_codes[r] = work.tile([P, GROUP * P], U32, name="e_codes", align_bytes=64)
+            e_scales[r] = work.tile([P, GROUP * P], U8, name="e_scales", align_bytes=64)
+            nc.vector.quantize_mx(out=e_codes[r][:].bitcast(FP8X4), scales=e_scales[r][:], in_=e_grouped[r][:])
+            c0 = r * GROUP
+            nc.vector.reciprocal(out=rinv[:, c0 : c0 + GROUP], in_=rowsum[:, c0 : c0 + GROUP])
+
+        def heads_matmul(r):
+            head_sums[r] = ps_heads.tile([P, GROUP, HD], F32, name="head_sums")
+            for a in range(GROUP):
+                kv = ((r % GROUPS) * GROUP + a) // 2
+                nc.tensor.matmul_mx(
+                    out=head_sums[r][:, a, :],
+                    lhsT=e_codes[r][:, a * P : (a + 1) * P].bitcast(FP8X4),
+                    lhsT_scale=e_scales[r][:, a * P : (a + 1) * P],
+                    rhs=v_codes[:, kv * HD : (kv + 1) * HD].bitcast(FP8X4),
+                    rhs_scale=v_scales[:, kv * HD : (kv + 1) * HD],
+                    start=True,
+                    stop=True,
                 )
 
-            for n in range(D // BANK):
-                cols = slice(n * BANK, (n + 1) * BANK)
-                acc = ps_out.tile([P, BANK], F32)
-                for g in range(GROUPS):
-                    nc.tensor.matmul_mx(
-                        out=acc[:],
-                        lhsT=o_codes[:, g, rows].bitcast(FP8X4),
-                        lhsT_scale=o_scales[:, g, rows],
-                        rhs=wo_codes[:, g, cols].bitcast(FP8X4),
-                        rhs_scale=wo_scales[:, g, cols],
-                        start=(g == 0),
-                        stop=(g == GROUPS - 1),
-                    )
-                result = work.tile([P, BANK], F32, bufs=4)
-                nc.vector.tensor_tensor(out=result[:], in0=acc[:], in1=x_sb[:, i, cols], op=ALU.add)
-                nc.sync.dma_start(out=out2[rows, cols], in_=result[:])
+        def normalise(r):
+            o_rows[r] = work.tile([P, GROUP * HD], BF16, name="o_rows")
+            for a in range(GROUP):
+                nc.scalar.activation(
+                    out=o_rows[r][:, a * HD : (a + 1) * HD],
+                    in_=head_sums[r][:, a, :],
+                    func=ACT.Copy,
+                    scale=rinv[:, r * GROUP + a : r * GROUP + a + 1],
+                )
+
+        def flip_o(r):
+            o_flips[r] = ps_flip.tile([P, 4, P], F32, name="flip")
+            words = o_rows[r][:].bitcast(F32)
+            for u in range(2):
+                nc.tensor.transpose(o_flips[r][:, u, :], words[:, u * P : (u + 1) * P], ident_f32[:])
+
+        def gather_o(r):
+            o_grouped[r] = work.tile([P, P * 4], BF16, name="o_grouped", align_bytes=64)
+            nc.scalar.copy(
+                out=o_grouped[r][:].bitcast(F32).rearrange("p (q u) -> p q u", u=2),
+                in_=o_flips[r][:, 0:2, :].rearrange("p u q -> p q u"),
+            )
+
+        def quantise_o(r):
+            i = tile_of_round(r)
+            g = r % GROUPS
+            rows = slice(i * P, (i + 1) * P)
+            nc.vector.quantize_mx(
+                out=o_codes[:, g, rows].bitcast(FP8X4), scales=o_scales[:, g, rows], in_=o_grouped[r][:]
+            )
+
+        wo_flips = {}
+        wo_grouped = {}
+
+        def flip_wo(item):
+            pr, g = divmod(item, GROUPS)
+            flip = ps_side.tile([P, 4, P], F32, name="side")
+            for r in range(2):
+                words = wo_raw[pr][:, r, :].bitcast(F32)
+                for u in range(2):
+                    w0 = 256 * g + 128 * u
+                    nc.tensor.transpose(flip[:, 2 * r + u, :], words[:, w0 : w0 + P], ident_f32[:])
+            wo_flips[item] = flip
+
+        def gather_wo(item):
+            wo_grouped[item] = work.tile([P, 4 * 2 * P], BF16, name="wo_grouped", align_bytes=64, bufs=3)
+            nc.scalar.copy(
+                out=wo_grouped[item][:].bitcast(F32).rearrange("p (r d u) -> p r d u", r=2, u=2),
+                in_=wo_flips[item][:].rearrange("p (r u) d -> p r d u", u=2),
+            )
+
+        def quantise_wo(item):
+            pr, g = divmod(item, GROUPS)
+            cols = slice(pr * 2 * P, (pr + 1) * 2 * P)
+            nc.vector.quantize_mx(
+                out=wo_codes[:, g, cols].bitcast(FP8X4), scales=wo_scales[:, g, cols], in_=wo_grouped[item][:]
+            )
+
+        sums = {}
+
+        def project(i, n):
+            rows = slice(i * P, (i + 1) * P)
+            cols = slice(n * BANK, (n + 1) * BANK)
+            acc = ps_side.tile([P, BANK], F32, name="side")
+            for g in range(GROUPS):
+                nc.tensor.matmul_mx(
+                    out=acc[:],
+                    lhsT=o_codes[:, g, rows].bitcast(FP8X4),
+                    lhsT_scale=o_scales[:, g, rows],
+                    rhs=wo_codes[:, g, cols].bitcast(FP8X4),
+                    rhs_scale=wo_scales[:, g, cols],
+                    start=(g == 0),
+                    stop=(g == GROUPS - 1),
+                )
+            sums[(i, n)] = acc
+
+        def add_residual(i, n):
+            rows = slice(i * P, (i + 1) * P)
+            cols = slice(n * BANK, (n + 1) * BANK)
+            result = work.tile([P, BANK], F32, name="result", bufs=4)
+            nc.vector.tensor_tensor(out=result[:], in0=sums[(i, n)][:], in1=x_sb[:, i, cols], op=ALU.add)
+            nc.sync.dma_start(out=out2[rows, cols], in_=result[:])
+
+        project_steps = {}
+        free_step = WO_STEP + WO_ITEMS + WO_QUANT_LAG + 1
+        for c in range(TILES):
+            start_step = max((c * GROUPS + GROUPS - 1 + 3) * GROUP + 2, free_step)
+            every = PROJECT_EVERY if c < TILES - 1 else 1
+            for n in range(BLOCKS):
+                project_steps[start_step + every * n] = (TILE_ORDER[c], n)
+            free_step = start_step + every * BLOCKS
+        last_step = max(project_steps) + RESIDUAL_LAG
+
+        for b in range(AHEAD):
+            issue_scores(b)
+        job_flips = {}
+        for step in range(last_step + 1):
+            r, a = divmod(step, GROUP)
+
+            if a == 0 and 0 <= r - 1 < ROUNDS:
+                flip_e(r - 1, 0)
+            if a == 2 and 0 <= r - 1 < ROUNDS:
+                flip_e(r - 1, 1)
+            if a == 1 and 0 <= r - 2 < ROUNDS:
+                heads_matmul(r - 2)
+            if a == 3 and 0 <= r - 2 < ROUNDS:
+                flip_o(r - 2)
+
+            if step in bank_at_step:
+                add_mask(step)
+                if bank_at_step[step] + AHEAD < len(banks):
+                    issue_scores(bank_at_step[step] + AHEAD)
+            if step - 1 in bank_at_step:
+                row_max(step - 1)
+
+            if 0 <= step - 2 < STEPS:
+                exponentials(step - 2)
+            if a == 1 and 0 <= r - 1 < ROUNDS:
+                gather_e(r - 1, 0)
+            if a == 3 and 0 <= r - 1 < ROUNDS:
+                gather_e(r - 1, 1)
+            if a == 2 and 0 <= r - 2 < ROUNDS:
+                normalise(r - 2)
+            if a == 0 and 0 <= r - 3 < ROUNDS:
+                gather_o(r - 3)
+
+            if a == 0 and 0 <= r - 2 < ROUNDS:
+                quantise_e(r - 2)
+            if a == 1 and 0 <= r - 3 < ROUNDS:
+                quantise_o(r - 3)
+
+            if step == V_STEP:
+                nc.vector.tensor_copy(out=v_grouped[:], in_=v_raw[:].rearrange("p u e c -> p c (u e)"))
+            if step == V_STEP + 1:
+                nc.vector.quantize_mx(
+                    out=v_codes[:].bitcast(FP8X4), scales=v_scales[:], in_=v_grouped[:].rearrange("p c t -> p (c t)")
+                )
+
+            job = step - FLIP_STEP
+            if 0 <= job < len(loop_jobs):
+                job_flips[job] = flip_heads(loop_jobs[job][0], loop_jobs[job][1])
+            if 0 <= job - 1 < len(loop_jobs):
+                nc.vector.tensor_copy(out=loop_jobs[job - 1][2], in_=job_flips[job - 1][:])
+
+            item = step - WO_STEP
+            if 0 <= item < WO_ITEMS:
+                flip_wo(item)
+                if item % GROUPS == GROUPS - 1 and item // GROUPS + WO_BUFS < WO_PAIRS:
+                    load_wo(item // GROUPS + WO_BUFS)
+            if 0 <= item - 1 < WO_ITEMS:
+                gather_wo(item - 1)
+            if 0 <= item - WO_QUANT_LAG < WO_ITEMS:
+                quantise_wo(item - WO_QUANT_LAG)
+
+            if step - RESIDUAL_LAG in project_steps:
+                add_residual(*project_steps[step - RESIDUAL_LAG])
+            if step in project_steps:
+                project(*project_steps[step])

@@ -25,7 +25,8 @@ GROUPS = H // GROUP
 BANK = 512
 BLOCKS = D // BANK
 E_TILES = 2 * GROUP
-SCALE = 1.0 / math.sqrt(HD)
+ROOT = math.sqrt(HD)
+SCALE = 1.0 / ROOT
 
 ROUNDS = TILES * GROUPS
 STEPS = ROUNDS * GROUP
@@ -36,7 +37,9 @@ TILE_ORDER = (0, 3, 2, 1)
 FLIP_STEP = 0
 V_STEP = 5
 WO_STEP = 7
-AHEAD = 2
+AHEAD = 1
+SCORE_BANKS = 3
+EXP_LAG = 1
 RESIDUAL_LAG = 2
 WO_QUANT_LAG = 3
 PROJECT_EVERY = 2
@@ -55,8 +58,8 @@ def tile_transformerblock_pb_kernel(tc, q_rot, k_rot, v, mask, wo, x, out):
     with ExitStack() as stack:
         fixed = stack.enter_context(tc.tile_pool(name="fixed", bufs=1))
         work = stack.enter_context(tc.tile_pool(name="work", bufs=2))
-        ps_scores = stack.enter_context(tc.psum_pool(name="ps_scores", bufs=AHEAD))
-        ps_flip = stack.enter_context(tc.psum_pool(name="ps_flip", bufs=3))
+        ps_scores = stack.enter_context(tc.psum_pool(name="ps_scores", bufs=SCORE_BANKS))
+        ps_flip = stack.enter_context(tc.psum_pool(name="ps_flip", bufs=2))
         ps_side = stack.enter_context(tc.psum_pool(name="ps_side", bufs=2))
         ps_heads = stack.enter_context(tc.psum_pool(name="ps_heads", bufs=1))
         stack.enter_context(tc.manual_schedule())
@@ -78,6 +81,8 @@ def tile_transformerblock_pb_kernel(tc, q_rot, k_rot, v, mask, wo, x, out):
         qT = fixed.tile([P, H, S], BF16)
         e_tiles = [fixed.tile([P, S], BF16, name="e%d" % n) for n in range(E_TILES)]
         e_filled = [S] * E_TILES
+        maskT = [fixed.tile([P, i + 1, P], F32, name="maskT%d" % i) for i in range(TILES)]
+        rawmax = fixed.tile([P, STEPS], F32)
         negmax = fixed.tile([P, STEPS], F32)
         rowsum = fixed.tile([P, STEPS], F32)
         rinv = fixed.tile([P, STEPS], F32)
@@ -122,31 +127,47 @@ def tile_transformerblock_pb_kernel(tc, q_rot, k_rot, v, mask, wo, x, out):
         make_identity(nc, ident_bf[:])
         make_identity(nc, ident_f32[:])
 
-        def flip_heads(raw, h0):
+        def flip_heads(raw, h0, count):
             flip = ps_flip.tile([P, 4, P], BF16, name="flip")
-            for c in range(4):
+            for c in range(count):
                 nc.tensor.transpose(flip[:, c, :], raw[:, (h0 + c) * HD : (h0 + c + 1) * HD], ident_bf[:])
             return flip
 
         def k_jobs(j):
-            return [(k_raw[j], h0, kT[:, h0 : h0 + 4, j * P : (j + 1) * P]) for h0 in range(0, KV, 4)]
+            return [(k_raw[j], h0, 4, kT[:, h0 : h0 + 4, j * P : (j + 1) * P], None) for h0 in range(0, KV, 4)]
 
         def q_jobs(i):
-            return [(q_raw[i], h0, qT[:, h0 : h0 + 4, i * P : (i + 1) * P]) for h0 in range(0, H, 4)]
+            return [(q_raw[i], h0, 4, qT[:, h0 : h0 + 4, i * P : (i + 1) * P], None) for h0 in range(0, H, 4)]
+
+        def mask_jobs(i):
+            return [(mask_sb[i], 0, i + 1, maskT[i][:], ROOT)]
 
         head_jobs = []
         loop_jobs = []
         for j in range(TILES):
             (head_jobs if j <= first else loop_jobs).extend(k_jobs(j))
+        head_jobs.extend(mask_jobs(first))
         head_jobs.extend(q_jobs(first))
         for i in TILE_ORDER[1:]:
+            loop_jobs.extend(mask_jobs(i))
             loop_jobs.extend(q_jobs(i))
-        for n, (raw, h0, dst) in enumerate(head_jobs):
-            flip = flip_heads(raw, h0)
-            if n % 2 == 0:
-                nc.scalar.copy(out=dst, in_=flip[:])
+
+        def finish_job(job, flip, on_scalar):
+            raw, h0, count, dst, factor = job
+            if factor is None:
+                if on_scalar:
+                    nc.scalar.copy(out=dst, in_=flip[:, 0:count, :])
+                else:
+                    nc.vector.tensor_copy(out=dst, in_=flip[:, 0:count, :])
+            elif on_scalar:
+                nc.scalar.activation(out=dst, in_=flip[:, 0:count, :], func=ACT.Copy, scale=factor)
             else:
-                nc.vector.tensor_copy(out=dst, in_=flip[:])
+                nc.vector.tensor_scalar(
+                    out=dst, in0=flip[:, 0:count, :], scalar1=factor, scalar2=None, op0=ALU.mult
+                )
+
+        for n, job in enumerate(head_jobs):
+            finish_job(job, flip_heads(*job[0:3]), n % 2 == 0)
 
         banks = []
         bank_at_step = {}
@@ -157,51 +178,52 @@ def tile_transformerblock_pb_kernel(tc, q_rot, k_rot, v, mask, wo, x, out):
                 bank_at_step[r * GROUP + a] = len(banks)
                 banks.append((i, (r % GROUPS) * GROUP + a, per_bank))
         score_tiles = {}
-        masked_banks = {}
-        masked_tiles = {}
+        head_scores = {}
 
         def issue_scores(b):
             i, h0, per_bank = banks[b]
             keys = keys_of(i)
             scores = ps_scores.tile([P, BANK], F32, name="scores")
             for a in range(per_bank):
+                for j in range(i + 1):
+                    nc.tensor.matmul(
+                        scores[:, a * keys + j * P : a * keys + (j + 1) * P],
+                        lhsT=maskT[i][:, j, :],
+                        rhs=ident_f32[:],
+                        start=(a == 0 and j == 0),
+                        stop=False,
+                        is_transpose=True,
+                    )
+            for a in range(per_bank):
                 nc.tensor.matmul(
                     scores[:, a * keys : (a + 1) * keys],
                     lhsT=qT[:, h0 + a, i * P : (i + 1) * P],
                     rhs=kT[:, (h0 + a) // 2, 0:keys],
-                    start=True,
-                    stop=True,
+                    start=False,
+                    stop=(a == per_bank - 1),
                 )
             score_tiles[b] = scores
 
-        def add_mask(step):
+        def row_max(step):
             b = bank_at_step[step]
             i, h0, per_bank = banks[b]
             keys = keys_of(i)
-            span = per_bank * keys
-            masked = work.tile([P, BANK], F32, name="masked", bufs=4)
-            nc.vector.scalar_tensor_tensor(
-                out=masked[:, 0:span].rearrange("p (a n) -> p a n", a=per_bank),
-                in0=score_tiles[b][:, 0:span].rearrange("p (a n) -> p a n", a=per_bank),
-                scalar=SCALE,
-                in1=mask_sb[i][:, 0:keys].unsqueeze(1).to_broadcast([P, per_bank, keys]),
-                op0=ALU.mult,
-                op1=ALU.add,
-            )
-            masked_banks[step] = masked
-            for a in range(per_bank):
-                masked_tiles[step + a] = masked[:, a * keys : (a + 1) * keys]
-
-        def row_max(step):
-            i, h0, per_bank = banks[bank_at_step[step]]
-            span = per_bank * keys_of(i)
             nc.vector.tensor_reduce(
-                out=negmax[:, step : step + per_bank],
-                in_=masked_banks[step][:, 0:span].rearrange("p (a n) -> p a n", a=per_bank),
+                out=rawmax[:, step : step + per_bank],
+                in_=score_tiles[b][:, 0 : per_bank * keys].rearrange("p (a n) -> p a n", a=per_bank),
                 axis=mybir.AxisListType.X,
                 op=ALU.max,
                 negate=True,
             )
+            nc.gpsimd.tensor_scalar(
+                out=negmax[:, step : step + per_bank],
+                in0=rawmax[:, step : step + per_bank],
+                scalar1=SCALE,
+                scalar2=None,
+                op0=ALU.mult,
+            )
+            for a in range(per_bank):
+                head_scores[step + a] = score_tiles[b][:, a * keys : (a + 1) * keys]
 
         def exponentials(step):
             keys = keys_of(tile_of_round(step // GROUP))
@@ -211,10 +233,10 @@ def tile_transformerblock_pb_kernel(tc, q_rot, k_rot, v, mask, wo, x, out):
             e_filled[n] = keys
             nc.scalar.activation(
                 out=e_tiles[n][:, 0:keys],
-                in_=masked_tiles[step],
+                in_=head_scores[step],
                 func=ACT.Exp,
                 bias=negmax[:, step : step + 1],
-                scale=1.0,
+                scale=SCALE,
                 accum_out=rowsum[:, step : step + 1],
             )
 
@@ -374,14 +396,11 @@ def tile_transformerblock_pb_kernel(tc, q_rot, k_rot, v, mask, wo, x, out):
                 flip_o(r - 2)
 
             if step in bank_at_step:
-                add_mask(step)
+                row_max(step)
                 if bank_at_step[step] + AHEAD < len(banks):
                     issue_scores(bank_at_step[step] + AHEAD)
-            if step - 1 in bank_at_step:
-                row_max(step - 1)
-
-            if 0 <= step - 2 < STEPS:
-                exponentials(step - 2)
+            if 0 <= step - EXP_LAG < STEPS:
+                exponentials(step - EXP_LAG)
             if a == 1 and 0 <= r - 1 < ROUNDS:
                 gather_e(r - 1, 0)
             if a == 3 and 0 <= r - 1 < ROUNDS:
@@ -405,9 +424,9 @@ def tile_transformerblock_pb_kernel(tc, q_rot, k_rot, v, mask, wo, x, out):
 
             job = step - FLIP_STEP
             if 0 <= job < len(loop_jobs):
-                job_flips[job] = flip_heads(loop_jobs[job][0], loop_jobs[job][1])
+                job_flips[job] = flip_heads(*loop_jobs[job][0:3])
             if 0 <= job - 1 < len(loop_jobs):
-                nc.vector.tensor_copy(out=loop_jobs[job - 1][2], in_=job_flips[job - 1][:])
+                finish_job(loop_jobs[job - 1], job_flips[job - 1], False)
 
             item = step - WO_STEP
             if 0 <= item < WO_ITEMS:

@@ -33,16 +33,33 @@ STEPS = ROUNDS * GROUP
 WO_PAIRS = D // (2 * P)
 WO_ITEMS = WO_PAIRS * GROUPS
 WO_BUFS = 4
-TILE_ORDER = (0, 3, 2, 1)
-FLIP_STEP = 0
-V_STEP = 5
-WO_STEP = 7
-AHEAD = 1
+TILE_ORDER = (3, 2, 1, 0)
 SCORE_BANKS = 3
-EXP_LAG = 1
-RESIDUAL_LAG = 2
+RING_BANKS = 5
+V_STEP = 4
+V_PARTS = 4
+VECTOR_WO_FROM = 8
+SCALAR_JOBS = 8
+WO_STEP = 2
 WO_QUANT_LAG = 3
-PROJECT_EVERY = 2
+VECTOR_WO = 3
+RESIDUAL_LAG = 2
+AHEAD = 1
+MASK_LEAD = 2
+E_FLIP = (3, 5)
+E_GATHER = (4, 6)
+E_QUANT = 7
+HEADS = 9
+NORMALISE = 10
+O_FLIP = 12
+O_GATHER = 13
+O_QUANT = 14
+TENSOR_MASK = (3, 2)
+WO_SPACING = 8
+WO_PER = 8
+PROJECT_LAG = 3
+HEAD_JOBS = 4
+DENSE_JOBS = 9
 
 FLOPS = 2 * (2 * H * S * S * HD) + 2 * S * D * NQ
 
@@ -59,9 +76,7 @@ def tile_transformerblock_pb_kernel(tc, q_rot, k_rot, v, mask, wo, x, out):
         fixed = stack.enter_context(tc.tile_pool(name="fixed", bufs=1))
         work = stack.enter_context(tc.tile_pool(name="work", bufs=2))
         ps_scores = stack.enter_context(tc.psum_pool(name="ps_scores", bufs=SCORE_BANKS))
-        ps_flip = stack.enter_context(tc.psum_pool(name="ps_flip", bufs=2))
-        ps_side = stack.enter_context(tc.psum_pool(name="ps_side", bufs=2))
-        ps_heads = stack.enter_context(tc.psum_pool(name="ps_heads", bufs=1))
+        ps_ring = stack.enter_context(tc.psum_pool(name="ps_ring", bufs=RING_BANKS))
         stack.enter_context(tc.manual_schedule())
 
         def tile_of_round(r):
@@ -70,7 +85,7 @@ def tile_transformerblock_pb_kernel(tc, q_rot, k_rot, v, mask, wo, x, out):
         def keys_of(i):
             return (i + 1) * P
 
-        k_raw = [fixed.tile([P, KV * HD], BF16, name="k_raw%d" % j) for j in range(TILES)]
+        k_raw = fixed.tile([P, TILES, KV * HD], BF16)
         q_raw = [fixed.tile([P, NQ], BF16, name="q_raw%d" % i) for i in range(TILES)]
         mask_sb = [fixed.tile([P, S], BF16, name="mask%d" % i) for i in range(TILES)]
         v_raw = fixed.tile([P, 2, 2, KV * HD], BF16)
@@ -81,9 +96,10 @@ def tile_transformerblock_pb_kernel(tc, q_rot, k_rot, v, mask, wo, x, out):
         qT = fixed.tile([P, H, S], BF16)
         e_tiles = [fixed.tile([P, S], BF16, name="e%d" % n) for n in range(E_TILES)]
         e_filled = [S] * E_TILES
-        maskT = [fixed.tile([P, i + 1, P], F32, name="maskT%d" % i) for i in range(TILES)]
+        maskT = {i: fixed.tile([P, i + 1, P], F32, name="maskT%d" % i) for i in TENSOR_MASK}
         rawmax = fixed.tile([P, STEPS], F32)
         negmax = fixed.tile([P, STEPS], F32)
+        negmax_v = fixed.tile([P, STEPS], F32)
         rowsum = fixed.tile([P, STEPS], F32)
         rinv = fixed.tile([P, STEPS], F32)
         v_grouped = fixed.tile([P, KV * HD, 4], BF16, align_bytes=64)
@@ -102,72 +118,88 @@ def tile_transformerblock_pb_kernel(tc, q_rot, k_rot, v, mask, wo, x, out):
                 out=wo_raw[pr][:], in_=wo[pr * 2 * P : (pr + 1) * 2 * P, :].rearrange("(r p) k -> p r k", p=P)
             )
 
-        def load_rows(dst, src, i):
-            nc.sync.dma_start(out=dst[i][:], in_=src[i * P : (i + 1) * P, :])
+        k_view = k2.rearrange("(j p) c -> p j c", p=P)
+        half_k = KV * HD // 2
+        half_q = NQ // 2
+
+        def load_k(part):
+            cols = slice(part * half_k, (part + 1) * half_k)
+            nc.sync.dma_start(out=k_raw[:, :, cols], in_=k_view[:, :, cols])
+
+        def load_q(i, part):
+            cols = slice(part * half_q, (part + 1) * half_q)
+            nc.sync.dma_start(out=q_raw[i][:, cols], in_=q2[i * P : (i + 1) * P, cols])
+
+        def load_mask(i):
+            nc.sync.dma_start(out=mask_sb[i][:], in_=mask[i * P : (i + 1) * P, :])
 
         first = TILE_ORDER[0]
-        for j in range(first + 1):
-            load_rows(k_raw, k2, j)
-        load_rows(mask_sb, mask, first)
-        load_rows(q_raw, q2, first)
-        for j in range(first + 1, TILES):
-            load_rows(k_raw, k2, j)
-        load_rows(mask_sb, mask, TILE_ORDER[1])
-        load_rows(q_raw, q2, TILE_ORDER[1])
-        nc.sync.dma_start(out=v_raw[:], in_=v2.rearrange("(u p e) c -> p u e c", u=2, e=2))
+        load_k(0)
+        load_q(first, 0)
+        load_mask(first)
+        load_k(1)
+        load_q(first, 1)
         load_wo(0)
+        nc.sync.dma_start(out=v_raw[:], in_=v2.rearrange("(u p e) c -> p u e c", u=2, e=2))
         load_wo(1)
-        for i in TILE_ORDER[2:]:
-            load_rows(mask_sb, mask, i)
-            load_rows(q_raw, q2, i)
-        load_wo(2)
+        for i in TILE_ORDER[1:]:
+            load_mask(i)
+            load_q(i, 0)
+            load_q(i, 1)
+            if i == TILE_ORDER[1]:
+                load_wo(2)
         load_wo(3)
         nc.sync.dma_start(out=x_sb[:], in_=x2.rearrange("(i p) d -> p i d", p=P))
 
         make_identity(nc, ident_bf[:])
         make_identity(nc, ident_f32[:])
 
-        def flip_heads(raw, h0, count):
-            flip = ps_flip.tile([P, 4, P], BF16, name="flip")
-            for c in range(count):
-                nc.tensor.transpose(flip[:, c, :], raw[:, (h0 + c) * HD : (h0 + c + 1) * HD], ident_bf[:])
+        def k_job(kv):
+            blocks = [k_raw[:, j, kv * HD : (kv + 1) * HD] for j in range(TILES)]
+            return (blocks, kT[:, kv, :].rearrange("p (j n) -> p j n", j=TILES), None)
+
+        def q_job(i, g):
+            h0 = g * GROUP
+            blocks = [q_raw[i][:, (h0 + a) * HD : (h0 + a + 1) * HD] for a in range(GROUP)]
+            return (blocks, qT[:, h0 : h0 + GROUP, i * P : (i + 1) * P], None)
+
+        def mask_job(i):
+            blocks = [mask_sb[i][:, j * P : (j + 1) * P] for j in range(i + 1)]
+            return (blocks, maskT[i][:], ROOT)
+
+        jobs = [mask_job(first), k_job(0), q_job(first, 0), k_job(1)]
+        for g in range(1, GROUPS):
+            jobs.extend([q_job(first, g), k_job(2 * g), k_job(2 * g + 1)])
+        for i in TILE_ORDER[1:]:
+            if i in TENSOR_MASK:
+                jobs.append(mask_job(i))
+            jobs.extend([q_job(i, g) for g in range(GROUPS)])
+
+        def flip_job(job):
+            flip = ps_ring.tile([P, 4, P], BF16, name="ring")
+            for c, block in enumerate(job[0]):
+                nc.tensor.transpose(flip[:, c, :], block, ident_bf[:])
             return flip
 
-        def k_jobs(j):
-            return [(k_raw[j], h0, 4, kT[:, h0 : h0 + 4, j * P : (j + 1) * P], None) for h0 in range(0, KV, 4)]
-
-        def q_jobs(i):
-            return [(q_raw[i], h0, 4, qT[:, h0 : h0 + 4, i * P : (i + 1) * P], None) for h0 in range(0, H, 4)]
-
-        def mask_jobs(i):
-            return [(mask_sb[i], 0, i + 1, maskT[i][:], ROOT)]
-
-        head_jobs = []
-        loop_jobs = []
-        for j in range(TILES):
-            (head_jobs if j <= first else loop_jobs).extend(k_jobs(j))
-        head_jobs.extend(mask_jobs(first))
-        head_jobs.extend(q_jobs(first))
-        for i in TILE_ORDER[1:]:
-            loop_jobs.extend(mask_jobs(i))
-            loop_jobs.extend(q_jobs(i))
-
         def finish_job(job, flip, on_scalar):
-            raw, h0, count, dst, factor = job
+            blocks, dst, factor = job
+            turned = flip[:, 0 : len(blocks), :]
             if factor is None:
                 if on_scalar:
-                    nc.scalar.copy(out=dst, in_=flip[:, 0:count, :])
+                    nc.scalar.copy(out=dst, in_=turned)
                 else:
-                    nc.vector.tensor_copy(out=dst, in_=flip[:, 0:count, :])
+                    nc.vector.tensor_copy(out=dst, in_=turned)
             elif on_scalar:
-                nc.scalar.activation(out=dst, in_=flip[:, 0:count, :], func=ACT.Copy, scale=factor)
+                nc.scalar.activation(out=dst, in_=turned, func=ACT.Copy, scale=factor)
             else:
-                nc.vector.tensor_scalar(
-                    out=dst, in0=flip[:, 0:count, :], scalar1=factor, scalar2=None, op0=ALU.mult
-                )
+                nc.vector.tensor_scalar(out=dst, in0=turned, scalar1=factor, scalar2=None, op0=ALU.mult)
 
-        for n, job in enumerate(head_jobs):
-            finish_job(job, flip_heads(*job[0:3]), n % 2 == 0)
+        for n in range(HEAD_JOBS):
+            finish_job(jobs[n], flip_job(jobs[n]), n % 2 == 0)
+        job_at_step = {}
+        for n in range(HEAD_JOBS, len(jobs)):
+            late = n - HEAD_JOBS - DENSE_JOBS
+            job_at_step[n - HEAD_JOBS if late < 0 else DENSE_JOBS + 1 + 2 * late] = jobs[n]
 
         banks = []
         bank_at_step = {}
@@ -185,7 +217,7 @@ def tile_transformerblock_pb_kernel(tc, q_rot, k_rot, v, mask, wo, x, out):
             keys = keys_of(i)
             scores = ps_scores.tile([P, BANK], F32, name="scores")
             for a in range(per_bank):
-                for j in range(i + 1):
+                for j in range(i + 1 if i in TENSOR_MASK else 0):
                     nc.tensor.matmul(
                         scores[:, a * keys + j * P : a * keys + (j + 1) * P],
                         lhsT=maskT[i][:, j, :],
@@ -199,34 +231,48 @@ def tile_transformerblock_pb_kernel(tc, q_rot, k_rot, v, mask, wo, x, out):
                     scores[:, a * keys : (a + 1) * keys],
                     lhsT=qT[:, h0 + a, i * P : (i + 1) * P],
                     rhs=kT[:, (h0 + a) // 2, 0:keys],
-                    start=False,
-                    stop=(a == per_bank - 1),
+                    start=(i not in TENSOR_MASK),
+                    stop=(i not in TENSOR_MASK or a == per_bank - 1),
                 )
             score_tiles[b] = scores
+
+        def add_mask(step):
+            b = bank_at_step[step]
+            i, h0, per_bank = banks[b]
+            keys = keys_of(i)
+            masked = work.tile([P, BANK], F32, name="masked", bufs=3)
+            nc.vector.scalar_tensor_tensor(
+                out=masked[:, 0 : per_bank * keys].rearrange("p (a n) -> p a n", a=per_bank),
+                in0=score_tiles[b][:, 0 : per_bank * keys].rearrange("p (a n) -> p a n", a=per_bank),
+                scalar=SCALE,
+                in1=mask_sb[i][:, 0:keys].unsqueeze(1).to_broadcast([P, per_bank, keys]),
+                op0=ALU.mult,
+                op1=ALU.add,
+            )
+            score_tiles[b] = masked
 
         def row_max(step):
             b = bank_at_step[step]
             i, h0, per_bank = banks[b]
             keys = keys_of(i)
+            cols = slice(step, step + per_bank)
             nc.vector.tensor_reduce(
-                out=rawmax[:, step : step + per_bank],
+                out=(rawmax if i in TENSOR_MASK else negmax_v)[:, cols],
                 in_=score_tiles[b][:, 0 : per_bank * keys].rearrange("p (a n) -> p a n", a=per_bank),
                 axis=mybir.AxisListType.X,
                 op=ALU.max,
                 negate=True,
             )
-            nc.gpsimd.tensor_scalar(
-                out=negmax[:, step : step + per_bank],
-                in0=rawmax[:, step : step + per_bank],
-                scalar1=SCALE,
-                scalar2=None,
-                op0=ALU.mult,
-            )
+            if i in TENSOR_MASK:
+                nc.gpsimd.tensor_scalar(
+                    out=negmax[:, cols], in0=rawmax[:, cols], scalar1=SCALE, scalar2=None, op0=ALU.mult
+                )
             for a in range(per_bank):
                 head_scores[step + a] = score_tiles[b][:, a * keys : (a + 1) * keys]
 
         def exponentials(step):
-            keys = keys_of(tile_of_round(step // GROUP))
+            i = tile_of_round(step // GROUP)
+            keys = keys_of(i)
             n = step % E_TILES
             if keys < e_filled[n]:
                 nc.gpsimd.memset(e_tiles[n][:, keys : e_filled[n]], 0.0)
@@ -235,8 +281,8 @@ def tile_transformerblock_pb_kernel(tc, q_rot, k_rot, v, mask, wo, x, out):
                 out=e_tiles[n][:, 0:keys],
                 in_=head_scores[step],
                 func=ACT.Exp,
-                bias=negmax[:, step : step + 1],
-                scale=SCALE,
+                bias=(negmax if i in TENSOR_MASK else negmax_v)[:, step : step + 1],
+                scale=SCALE if i in TENSOR_MASK else 1.0,
                 accum_out=rowsum[:, step : step + 1],
             )
 
@@ -250,7 +296,7 @@ def tile_transformerblock_pb_kernel(tc, q_rot, k_rot, v, mask, wo, x, out):
         o_grouped = {}
 
         def flip_e(r, half):
-            flip = ps_flip.tile([P, 4, P], F32, name="flip")
+            flip = ps_ring.tile([P, 4, P], F32, name="ring")
             for a in range(2):
                 words = e_tiles[(r * GROUP + 2 * half + a) % E_TILES][:].bitcast(F32)
                 for u in range(2):
@@ -274,7 +320,7 @@ def tile_transformerblock_pb_kernel(tc, q_rot, k_rot, v, mask, wo, x, out):
             nc.vector.reciprocal(out=rinv[:, c0 : c0 + GROUP], in_=rowsum[:, c0 : c0 + GROUP])
 
         def heads_matmul(r):
-            head_sums[r] = ps_heads.tile([P, GROUP, HD], F32, name="head_sums")
+            head_sums[r] = ps_ring.tile([P, GROUP, HD], F32, name="ring")
             for a in range(GROUP):
                 kv = ((r % GROUPS) * GROUP + a) // 2
                 nc.tensor.matmul_mx(
@@ -298,7 +344,7 @@ def tile_transformerblock_pb_kernel(tc, q_rot, k_rot, v, mask, wo, x, out):
                 )
 
         def flip_o(r):
-            o_flips[r] = ps_flip.tile([P, 4, P], F32, name="flip")
+            o_flips[r] = ps_ring.tile([P, 4, P], F32, name="ring")
             words = o_rows[r][:].bitcast(F32)
             for u in range(2):
                 nc.tensor.transpose(o_flips[r][:, u, :], words[:, u * P : (u + 1) * P], ident_f32[:])
@@ -323,7 +369,7 @@ def tile_transformerblock_pb_kernel(tc, q_rot, k_rot, v, mask, wo, x, out):
 
         def flip_wo(item):
             pr, g = divmod(item, GROUPS)
-            flip = ps_side.tile([P, 4, P], F32, name="side")
+            flip = ps_ring.tile([P, 4, P], F32, name="ring")
             for r in range(2):
                 words = wo_raw[pr][:, r, :].bitcast(F32)
                 for u in range(2):
@@ -333,10 +379,12 @@ def tile_transformerblock_pb_kernel(tc, q_rot, k_rot, v, mask, wo, x, out):
 
         def gather_wo(item):
             wo_grouped[item] = work.tile([P, 4 * 2 * P], BF16, name="wo_grouped", align_bytes=64, bufs=3)
-            nc.scalar.copy(
-                out=wo_grouped[item][:].bitcast(F32).rearrange("p (r d u) -> p r d u", r=2, u=2),
-                in_=wo_flips[item][:].rearrange("p (r u) d -> p r d u", u=2),
-            )
+            dst = wo_grouped[item][:].bitcast(F32).rearrange("p (r d u) -> p r d u", r=2, u=2)
+            src = wo_flips[item][:].rearrange("p (r u) d -> p r d u", u=2)
+            if item >= VECTOR_WO_FROM and item % VECTOR_WO == VECTOR_WO - 1:
+                nc.vector.tensor_copy(out=dst, in_=src)
+            else:
+                nc.scalar.copy(out=dst, in_=src)
 
         def quantise_wo(item):
             pr, g = divmod(item, GROUPS)
@@ -347,13 +395,17 @@ def tile_transformerblock_pb_kernel(tc, q_rot, k_rot, v, mask, wo, x, out):
 
         sums = {}
 
-        def project(i, n):
+        def project(i, n, groups):
             rows = slice(i * P, (i + 1) * P)
             cols = slice(n * BANK, (n + 1) * BANK)
-            acc = ps_side.tile([P, BANK], F32, name="side")
-            for g in range(GROUPS):
+            if groups[0] == 0:
+                if i == TILE_ORDER[-1] and n < SCORE_BANKS:
+                    sums[(i, n)] = ps_scores.tile([P, BANK], F32, name="scores")
+                else:
+                    sums[(i, n)] = ps_ring.tile([P, BANK], F32, name="ring")
+            for g in groups:
                 nc.tensor.matmul_mx(
-                    out=acc[:],
+                    out=sums[(i, n)][:],
                     lhsT=o_codes[:, g, rows].bitcast(FP8X4),
                     lhsT_scale=o_scales[:, g, rows],
                     rhs=wo_codes[:, g, cols].bitcast(FP8X4),
@@ -361,7 +413,6 @@ def tile_transformerblock_pb_kernel(tc, q_rot, k_rot, v, mask, wo, x, out):
                     start=(g == 0),
                     stop=(g == GROUPS - 1),
                 )
-            sums[(i, n)] = acc
 
         def add_residual(i, n):
             rows = slice(i * P, (i + 1) * P)
@@ -371,74 +422,96 @@ def tile_transformerblock_pb_kernel(tc, q_rot, k_rot, v, mask, wo, x, out):
             nc.sync.dma_start(out=out2[rows, cols], in_=result[:])
 
         project_steps = {}
-        free_step = WO_STEP + WO_ITEMS + WO_QUANT_LAG + 1
-        for c in range(TILES):
-            start_step = max((c * GROUPS + GROUPS - 1 + 3) * GROUP + 2, free_step)
-            every = PROJECT_EVERY if c < TILES - 1 else 1
-            for n in range(BLOCKS):
-                project_steps[start_step + every * n] = (TILE_ORDER[c], n)
-            free_step = start_step + every * BLOCKS
-        last_step = max(project_steps) + RESIDUAL_LAG
+        residual_steps = {}
+        whole = tuple(range(GROUPS))
 
-        for b in range(AHEAD):
+        def plan(step, i, n, groups):
+            project_steps.setdefault(step, []).append((i, n, groups))
+            if groups[-1] == GROUPS - 1:
+                residual_steps.setdefault(step + RESIDUAL_LAG, []).append((i, n))
+
+        for c in range(TILES - 1):
+            for n in range(BLOCKS):
+                plan((c * GROUPS + GROUPS + PROJECT_LAG + n) * GROUP + HEADS % GROUP, TILE_ORDER[c], n, whole)
+        o_done = (ROUNDS - 1) * GROUP + O_QUANT
+        for n in range(BLOCKS):
+            plan(o_done - 3 + n, TILE_ORDER[-1], n, whole[:-1])
+            plan(o_done + 1, TILE_ORDER[-1], n, whole[-1:])
+        last_step = max(residual_steps)
+
+        def item_at(step):
+            t = step - WO_STEP
+            if t < 0 or t % WO_SPACING >= WO_PER:
+                return None
+            item = t // WO_SPACING * WO_PER + t % WO_SPACING
+            return item if item < WO_ITEMS else None
+
+        def rounds_at(step, offset):
+            r, a = divmod(step - offset, GROUP)
+            return [r] if a == 0 and 0 <= r < ROUNDS else []
+
+        issue_at_step = {}
+        for first_head, b in bank_at_step.items():
+            early = AHEAD if banks[b][0] in TENSOR_MASK else AHEAD + MASK_LEAD
+            issue_at_step.setdefault(first_head - early, []).append(b)
+        for b in issue_at_step[-AHEAD]:
             issue_scores(b)
         job_flips = {}
         for step in range(last_step + 1):
-            r, a = divmod(step, GROUP)
+            item = item_at(step)
 
-            if a == 0 and 0 <= r - 1 < ROUNDS:
-                flip_e(r - 1, 0)
-            if a == 2 and 0 <= r - 1 < ROUNDS:
-                flip_e(r - 1, 1)
-            if a == 1 and 0 <= r - 2 < ROUNDS:
-                heads_matmul(r - 2)
-            if a == 3 and 0 <= r - 2 < ROUNDS:
-                flip_o(r - 2)
-
-            if step in bank_at_step:
+            ahead = step + MASK_LEAD
+            if ahead in bank_at_step and banks[bank_at_step[ahead]][0] not in TENSOR_MASK:
+                add_mask(ahead)
+                row_max(ahead)
+            if step in bank_at_step and banks[bank_at_step[step]][0] in TENSOR_MASK:
                 row_max(step)
-                if bank_at_step[step] + AHEAD < len(banks):
-                    issue_scores(bank_at_step[step] + AHEAD)
-            if 0 <= step - EXP_LAG < STEPS:
-                exponentials(step - EXP_LAG)
-            if a == 1 and 0 <= r - 1 < ROUNDS:
-                gather_e(r - 1, 0)
-            if a == 3 and 0 <= r - 1 < ROUNDS:
-                gather_e(r - 1, 1)
-            if a == 2 and 0 <= r - 2 < ROUNDS:
-                normalise(r - 2)
-            if a == 0 and 0 <= r - 3 < ROUNDS:
-                gather_o(r - 3)
+            if 0 <= step - 1 < STEPS:
+                exponentials(step - 1)
 
-            if a == 0 and 0 <= r - 2 < ROUNDS:
-                quantise_e(r - 2)
-            if a == 1 and 0 <= r - 3 < ROUNDS:
-                quantise_o(r - 3)
+            for half in range(2):
+                for r in rounds_at(step, E_GATHER[half]):
+                    gather_e(r, half)
+            for r in rounds_at(step, NORMALISE):
+                normalise(r)
+            for r in rounds_at(step, O_GATHER):
+                gather_o(r)
 
-            if step == V_STEP:
-                nc.vector.tensor_copy(out=v_grouped[:], in_=v_raw[:].rearrange("p u e c -> p c (u e)"))
-            if step == V_STEP + 1:
+            if step - 1 in job_at_step:
+                finish_job(job_at_step[step - 1], job_flips[step - 1], step < SCALAR_JOBS and step % 2 == 0)
+            for r in rounds_at(step, E_QUANT):
+                quantise_e(r)
+            for r in rounds_at(step, O_QUANT):
+                quantise_o(r)
+            if V_STEP <= step < V_STEP + V_PARTS:
+                width = KV * HD // V_PARTS
+                part = slice((step - V_STEP) * width, (step - V_STEP + 1) * width)
+                nc.vector.tensor_copy(out=v_grouped[:, part, :], in_=v_raw[:, :, :, part].rearrange("p u e c -> p c (u e)"))
+            if step == V_STEP + V_PARTS:
                 nc.vector.quantize_mx(
                     out=v_codes[:].bitcast(FP8X4), scales=v_scales[:], in_=v_grouped[:].rearrange("p c t -> p (c t)")
                 )
+            if item_at(step - 1) is not None:
+                gather_wo(item_at(step - 1))
+            if item_at(step - WO_QUANT_LAG) is not None:
+                quantise_wo(item_at(step - WO_QUANT_LAG))
+            for block in residual_steps.get(step, ()):
+                add_residual(*block)
 
-            job = step - FLIP_STEP
-            if 0 <= job < len(loop_jobs):
-                job_flips[job] = flip_heads(*loop_jobs[job][0:3])
-            if 0 <= job - 1 < len(loop_jobs):
-                finish_job(loop_jobs[job - 1], job_flips[job - 1], False)
-
-            item = step - WO_STEP
-            if 0 <= item < WO_ITEMS:
+            for b in issue_at_step.get(step, ()):
+                issue_scores(b)
+            for half in range(2):
+                for r in rounds_at(step, E_FLIP[half]):
+                    flip_e(r, half)
+            for r in rounds_at(step, O_FLIP):
+                flip_o(r)
+            if step in job_at_step:
+                job_flips[step] = flip_job(job_at_step[step])
+            if item is not None:
                 flip_wo(item)
                 if item % GROUPS == GROUPS - 1 and item // GROUPS + WO_BUFS < WO_PAIRS:
                     load_wo(item // GROUPS + WO_BUFS)
-            if 0 <= item - 1 < WO_ITEMS:
-                gather_wo(item - 1)
-            if 0 <= item - WO_QUANT_LAG < WO_ITEMS:
-                quantise_wo(item - WO_QUANT_LAG)
-
-            if step - RESIDUAL_LAG in project_steps:
-                add_residual(*project_steps[step - RESIDUAL_LAG])
-            if step in project_steps:
-                project(*project_steps[step])
+            for r in rounds_at(step, HEADS):
+                heads_matmul(r)
+            for block in project_steps.get(step, ()):
+                project(*block)

@@ -7,12 +7,14 @@ from concourse.masks import make_identity
 BF16 = mybir.dt.bfloat16
 F32 = mybir.dt.float32
 U32 = mybir.dt.uint32
+I32 = mybir.dt.int32
 U8 = mybir.dt.uint8
 FP8X4 = mybir.dt.float8_e4m3fn_x4
 ALU = mybir.AluOpType
 ACT = mybir.ActivationFunctionType
 
 P = 128
+HALF = P // 2
 S = 512
 H = 16
 KV = 8
@@ -37,7 +39,9 @@ TILE_ORDER = (3, 2, 1, 0)
 SCORE_BANKS = 3
 RING_BANKS = 5
 V_STEP = 4
-V_PARTS = 4
+VP_STEP = 12
+PAIRED = (1, 0)
+V_PARTS = 8
 VECTOR_WO_FROM = 8
 SCALAR_JOBS = 8
 WO_STEP = 2
@@ -54,12 +58,13 @@ NORMALISE = 10
 O_FLIP = 12
 O_GATHER = 13
 O_QUANT = 14
-TENSOR_MASK = (3, 2)
+TENSOR_MASK = (3, 2, 1)
 WO_SPACING = 8
 WO_PER = 8
-PROJECT_LAG = 3
-HEAD_JOBS = 4
-DENSE_JOBS = 9
+PROJECT_PLAN = {3: (8, 1), 2: (12, 1), 1: (16, 2)}
+WARM_MATMULS = 5
+HEAD_JOBS = 3
+DENSE_JOBS = 10
 
 FLOPS = 2 * (2 * H * S * S * HD) + 2 * S * D * NQ
 
@@ -88,7 +93,6 @@ def tile_transformerblock_pb_kernel(tc, q_rot, k_rot, v, mask, wo, x, out):
         k_raw = fixed.tile([P, TILES, KV * HD], BF16)
         q_raw = [fixed.tile([P, NQ], BF16, name="q_raw%d" % i) for i in range(TILES)]
         mask_sb = [fixed.tile([P, S], BF16, name="mask%d" % i) for i in range(TILES)]
-        v_raw = fixed.tile([P, 2, 2, KV * HD], BF16)
         x_sb = fixed.tile([P, TILES, D], BF16)
         ident_bf = fixed.tile([P, P], BF16)
         ident_f32 = fixed.tile([P, P], F32)
@@ -102,9 +106,11 @@ def tile_transformerblock_pb_kernel(tc, q_rot, k_rot, v, mask, wo, x, out):
         negmax_v = fixed.tile([P, STEPS], F32)
         rowsum = fixed.tile([P, STEPS], F32)
         rinv = fixed.tile([P, STEPS], F32)
-        v_grouped = fixed.tile([P, KV * HD, 4], BF16, align_bytes=64)
         v_codes = fixed.tile([P, KV * HD], U32, align_bytes=64)
         v_scales = fixed.tile([P, KV * HD], U8, align_bytes=64)
+        vp_codes = fixed.tile([P, KV * HD], U32, align_bytes=64)
+        vp_scales = fixed.tile([P, KV * HD], U8, align_bytes=64)
+        vp_half = fixed.tile([P, 2, KV * HD], U32, align_bytes=64)
         wo_codes = fixed.tile([P, GROUPS, D], U32, align_bytes=64)
         wo_scales = fixed.tile([P, GROUPS, D], U8, align_bytes=64)
         o_codes = fixed.tile([P, GROUPS, S], U32, align_bytes=64)
@@ -119,38 +125,51 @@ def tile_transformerblock_pb_kernel(tc, q_rot, k_rot, v, mask, wo, x, out):
             )
 
         k_view = k2.rearrange("(j p) c -> p j c", p=P)
-        half_k = KV * HD // 2
-        half_q = NQ // 2
 
-        def load_k(part):
-            cols = slice(part * half_k, (part + 1) * half_k)
+        def load_k(kv, count):
+            cols = slice(kv * HD, (kv + count) * HD)
             nc.sync.dma_start(out=k_raw[:, :, cols], in_=k_view[:, :, cols])
 
-        def load_q(i, part):
-            cols = slice(part * half_q, (part + 1) * half_q)
+        def load_q(i, h, count):
+            cols = slice(h * HD, (h + count) * HD)
             nc.sync.dma_start(out=q_raw[i][:, cols], in_=q2[i * P : (i + 1) * P, cols])
 
         def load_mask(i):
             nc.sync.dma_start(out=mask_sb[i][:], in_=mask[i * P : (i + 1) * P, :])
 
+        def load_vp():
+            v_raw[1] = fixed.tile([P, 2, 2, KV * HD], BF16, name="v_raw")
+            for h in range(2):
+                nc.sync.dma_start(
+                    out=v_raw[1][h * HALF : (h + 1) * HALF], in_=v2[0 : 2 * P, :].rearrange("(u p e) c -> p u e c", u=2, e=2)
+                )
+
         first = TILE_ORDER[0]
-        load_k(0)
-        load_q(first, 0)
         load_mask(first)
-        load_k(1)
-        load_q(first, 1)
+        load_k(0, 2)
+        load_q(first, 0, GROUP)
+        load_q(first, GROUP, GROUP)
+        load_k(2, 2)
+        load_k(4, KV - 4)
+        load_q(first, 2 * GROUP, H - 2 * GROUP)
         load_wo(0)
-        nc.sync.dma_start(out=v_raw[:], in_=v2.rearrange("(u p e) c -> p u e c", u=2, e=2))
+        v_raw = {}
+        v_raw[0] = fixed.tile([P, 2, 2, KV * HD], BF16, name="v_raw")
+        nc.sync.dma_start(out=v_raw[0][:], in_=v2.rearrange("(u p e) c -> p u e c", u=2, e=2))
         load_wo(1)
         for i in TILE_ORDER[1:]:
             load_mask(i)
-            load_q(i, 0)
-            load_q(i, 1)
+            load_q(i, 0, H)
             if i == TILE_ORDER[1]:
                 load_wo(2)
+                load_vp()
         load_wo(3)
         nc.sync.dma_start(out=x_sb[:], in_=x2.rearrange("(i p) d -> p i d", p=P))
 
+        nc.gpsimd.memset(vp_half[:], 0)
+
+        warm = fixed.tile([P, BANK], BF16)
+        nc.vector.memset(warm[:], 0.0)
         make_identity(nc, ident_bf[:])
         make_identity(nc, ident_f32[:])
 
@@ -178,7 +197,7 @@ def tile_transformerblock_pb_kernel(tc, q_rot, k_rot, v, mask, wo, x, out):
         def flip_job(job):
             flip = ps_ring.tile([P, 4, P], BF16, name="ring")
             for c, block in enumerate(job[0]):
-                nc.tensor.transpose(flip[:, c, :], block, ident_bf[:])
+                nc.tensor.matmul(flip[:, c, :], lhsT=block, rhs=ident_bf[:], start=True, stop=True)
             return flip
 
         def finish_job(job, flip, on_scalar):
@@ -193,6 +212,10 @@ def tile_transformerblock_pb_kernel(tc, q_rot, k_rot, v, mask, wo, x, out):
                 nc.scalar.activation(out=dst, in_=turned, func=ACT.Copy, scale=factor)
             else:
                 nc.vector.tensor_scalar(out=dst, in0=turned, scalar1=factor, scalar2=None, op0=ALU.mult)
+
+        warm_sums = ps_ring.tile([P, BANK], F32, name="ring")
+        for n in range(WARM_MATMULS):
+            nc.tensor.matmul(warm_sums[:], lhsT=warm[:, 0:P], rhs=warm[:], start=True, stop=True)
 
         for n in range(HEAD_JOBS):
             finish_job(jobs[n], flip_job(jobs[n]), n % 2 == 0)
@@ -273,13 +296,23 @@ def tile_transformerblock_pb_kernel(tc, q_rot, k_rot, v, mask, wo, x, out):
         def exponentials(step):
             i = tile_of_round(step // GROUP)
             keys = keys_of(i)
-            n = step % E_TILES
-            if keys < e_filled[n]:
-                nc.gpsimd.memset(e_tiles[n][:, keys : e_filled[n]], 0.0)
-            e_filled[n] = keys
+            if i in PAIRED:
+                n = step // 2 % E_TILES
+                used = i + 1
+                dst = e_tiles[n][:].rearrange("p (u h k) -> p h u k", u=2, h=2)[:, step % 2, 0:used, :]
+                src = head_scores[step].rearrange("p (u k) -> p u k", k=P)
+                filled = 2 * keys
+            else:
+                n = step % E_TILES
+                dst = e_tiles[n][:, 0:keys]
+                src = head_scores[step]
+                filled = keys
+            if filled < e_filled[n]:
+                nc.gpsimd.memset(e_tiles[n][:, filled : e_filled[n]], 0.0)
+            e_filled[n] = filled
             nc.scalar.activation(
-                out=e_tiles[n][:, 0:keys],
-                in_=head_scores[step],
+                out=dst,
+                in_=src,
                 func=ACT.Exp,
                 bias=(negmax if i in TENSOR_MASK else negmax_v)[:, step : step + 1],
                 scale=SCALE if i in TENSOR_MASK else 1.0,
@@ -296,39 +329,51 @@ def tile_transformerblock_pb_kernel(tc, q_rot, k_rot, v, mask, wo, x, out):
         o_grouped = {}
 
         def flip_e(r, half):
+            paired = tile_of_round(r) in PAIRED
             flip = ps_ring.tile([P, 4, P], F32, name="ring")
             for a in range(2):
-                words = e_tiles[(r * GROUP + 2 * half + a) % E_TILES][:].bitcast(F32)
+                n = 2 * r + a if paired else r * GROUP + 2 * half + a
+                words = e_tiles[n % E_TILES][:].bitcast(F32)
                 for u in range(2):
                     nc.tensor.transpose(flip[:, 2 * a + u, :], words[:, u * P : (u + 1) * P], ident_f32[:])
             e_flips[(r, half)] = flip
 
         def gather_e(r, half):
-            if half == 0:
+            paired = tile_of_round(r) in PAIRED
+            if r not in e_grouped:
                 e_grouped[r] = work.tile([P, GROUP * P * 4], BF16, name="e_grouped", align_bytes=64)
             e_words = e_grouped[r][:].bitcast(F32).rearrange("p (a q u) -> p a q u", a=GROUP, u=2)
+            a0 = 0 if paired else 2 * half
             nc.scalar.copy(
-                out=e_words[:, 2 * half : 2 * half + 2],
-                in_=e_flips[(r, half)][:].rearrange("p (a u) q -> p a q u", u=2),
+                out=e_words[:, a0 : a0 + 2], in_=e_flips[(r, half)][:].rearrange("p (a u) q -> p a q u", u=2)
             )
 
         def quantise_e(r):
+            columns = P * (GROUP // 2 if tile_of_round(r) in PAIRED else GROUP)
             e_codes[r] = work.tile([P, GROUP * P], U32, name="e_codes", align_bytes=64)
             e_scales[r] = work.tile([P, GROUP * P], U8, name="e_scales", align_bytes=64)
-            nc.vector.quantize_mx(out=e_codes[r][:].bitcast(FP8X4), scales=e_scales[r][:], in_=e_grouped[r][:])
+            nc.vector.quantize_mx(
+                out=e_codes[r][:, 0:columns].bitcast(FP8X4),
+                scales=e_scales[r][:, 0:columns],
+                in_=e_grouped[r][:, 0 : 4 * columns],
+            )
             c0 = r * GROUP
             nc.vector.reciprocal(out=rinv[:, c0 : c0 + GROUP], in_=rowsum[:, c0 : c0 + GROUP])
 
         def heads_matmul(r):
+            paired = tile_of_round(r) in PAIRED
             head_sums[r] = ps_ring.tile([P, GROUP, HD], F32, name="ring")
             for a in range(GROUP):
                 kv = ((r % GROUPS) * GROUP + a) // 2
+                queries = slice((a // 2 if paired else a) * P, (a // 2 + 1 if paired else a + 1) * P)
+                features = slice(kv * HD, (kv + 1) * HD)
+                codes, scales = (vp_half[:, a % 2, :], vp_scales) if paired else (v_codes[:], v_scales)
                 nc.tensor.matmul_mx(
                     out=head_sums[r][:, a, :],
-                    lhsT=e_codes[r][:, a * P : (a + 1) * P].bitcast(FP8X4),
-                    lhsT_scale=e_scales[r][:, a * P : (a + 1) * P],
-                    rhs=v_codes[:, kv * HD : (kv + 1) * HD].bitcast(FP8X4),
-                    rhs_scale=v_scales[:, kv * HD : (kv + 1) * HD],
+                    lhsT=e_codes[r][:, queries].bitcast(FP8X4),
+                    lhsT_scale=e_scales[r][:, queries],
+                    rhs=codes[:, features].bitcast(FP8X4),
+                    rhs_scale=scales[:, features],
                     start=True,
                     stop=True,
                 )
@@ -363,6 +408,33 @@ def tile_transformerblock_pb_kernel(tc, q_rot, k_rot, v, mask, wo, x, out):
             nc.vector.quantize_mx(
                 out=o_codes[:, g, rows].bitcast(FP8X4), scales=o_scales[:, g, rows], in_=o_grouped[r][:]
             )
+
+        v_grouped = {}
+
+        def interleave_v(which, n, engine):
+            if n == 0:
+                v_grouped[which] = fixed.tile([P, KV * HD, 4], BF16, name="v_grouped", align_bytes=64)
+            width = KV * HD // V_PARTS
+            part = slice(n * width, (n + 1) * width)
+            engine.tensor_scalar(
+                out=v_grouped[which][:, part, :],
+                in0=v_raw[which][:, :, :, part].rearrange("p u e c -> p c (u e)"),
+                scalar1=1.0,
+                scalar2=0.0,
+                op0=ALU.mult,
+                op1=ALU.add,
+            )
+
+        def quantise_v(which):
+            codes, scales = ((v_codes, v_scales), (vp_codes, vp_scales))[which]
+            nc.vector.quantize_mx(
+                out=codes[:].bitcast(FP8X4), scales=scales[:], in_=v_grouped[which][:].rearrange("p c t -> p (c t)")
+            )
+
+        def spread_vp():
+            for h in range(2):
+                rows = slice(h * HALF, (h + 1) * HALF)
+                nc.vector.tensor_copy(out=vp_half[rows, h, :].bitcast(I32), in_=vp_codes[rows, :].bitcast(I32))
 
         wo_flips = {}
         wo_grouped = {}
@@ -430,9 +502,9 @@ def tile_transformerblock_pb_kernel(tc, q_rot, k_rot, v, mask, wo, x, out):
             if groups[-1] == GROUPS - 1:
                 residual_steps.setdefault(step + RESIDUAL_LAG, []).append((i, n))
 
-        for c in range(TILES - 1):
+        for i, (first_round, per_round) in PROJECT_PLAN.items():
             for n in range(BLOCKS):
-                plan((c * GROUPS + GROUPS + PROJECT_LAG + n) * GROUP + HEADS % GROUP, TILE_ORDER[c], n, whole)
+                plan((first_round + n // per_round) * GROUP + HEADS % GROUP, i, n, whole)
         o_done = (ROUNDS - 1) * GROUP + O_QUANT
         for n in range(BLOCKS):
             plan(o_done - 3 + n, TILE_ORDER[-1], n, whole[:-1])
@@ -471,7 +543,8 @@ def tile_transformerblock_pb_kernel(tc, q_rot, k_rot, v, mask, wo, x, out):
 
             for half in range(2):
                 for r in rounds_at(step, E_GATHER[half]):
-                    gather_e(r, half)
+                    if half == 1 or tile_of_round(r) not in PAIRED:
+                        gather_e(r, half)
             for r in rounds_at(step, NORMALISE):
                 normalise(r)
             for r in rounds_at(step, O_GATHER):
@@ -483,14 +556,17 @@ def tile_transformerblock_pb_kernel(tc, q_rot, k_rot, v, mask, wo, x, out):
                 quantise_e(r)
             for r in rounds_at(step, O_QUANT):
                 quantise_o(r)
-            if V_STEP <= step < V_STEP + V_PARTS:
-                width = KV * HD // V_PARTS
-                part = slice((step - V_STEP) * width, (step - V_STEP + 1) * width)
-                nc.vector.tensor_copy(out=v_grouped[:, part, :], in_=v_raw[:, :, :, part].rearrange("p u e c -> p c (u e)"))
-            if step == V_STEP + V_PARTS:
-                nc.vector.quantize_mx(
-                    out=v_codes[:].bitcast(FP8X4), scales=v_scales[:], in_=v_grouped[:].rearrange("p c t -> p (c t)")
-                )
+            for n in range(V_PARTS):
+                if step == V_STEP + n // 2:
+                    interleave_v(0, n, nc.vector if n % 2 == 0 else nc.gpsimd)
+                if step == VP_STEP + 2 * n:
+                    interleave_v(1, n, nc.gpsimd)
+            if step == V_STEP + V_PARTS // 2:
+                quantise_v(0)
+            if step == VP_STEP + 2 * V_PARTS:
+                quantise_v(1)
+            if step == VP_STEP + 2 * V_PARTS + 2:
+                spread_vp()
             if item_at(step - 1) is not None:
                 gather_wo(item_at(step - 1))
             if item_at(step - WO_QUANT_LAG) is not None:
@@ -502,7 +578,8 @@ def tile_transformerblock_pb_kernel(tc, q_rot, k_rot, v, mask, wo, x, out):
                 issue_scores(b)
             for half in range(2):
                 for r in rounds_at(step, E_FLIP[half]):
-                    flip_e(r, half)
+                    if half == 1 or tile_of_round(r) not in PAIRED:
+                        flip_e(r, half)
             for r in rounds_at(step, O_FLIP):
                 flip_o(r)
             if step in job_at_step:

@@ -48,6 +48,8 @@ WO_STEP = 2
 WO_QUANT_LAG = 3
 VECTOR_WO = 3
 RESIDUAL_LAG = 2
+X_STEP = 22
+KEPT_BACK = 2
 AHEAD = 1
 MASK_LEAD = 2
 E_FLIP = (3, 5)
@@ -58,13 +60,14 @@ NORMALISE = 10
 O_FLIP = 12
 O_GATHER = 13
 O_QUANT = 14
-TENSOR_MASK = (3, 2, 1)
+VECTOR_MASK_ROUND = 10
 WO_SPACING = 8
-WO_PER = 8
+WO_PER = 7
 PROJECT_PLAN = {3: (8, 1), 2: (12, 1), 1: (16, 2)}
 WARM_MATMULS = 5
 HEAD_JOBS = 3
 DENSE_JOBS = 10
+TENSOR_MASK_TILES = TILE_ORDER[: -(-VECTOR_MASK_ROUND // GROUPS)]
 
 FLOPS = 2 * (2 * H * S * S * HD) + 2 * S * D * NQ
 
@@ -100,7 +103,7 @@ def tile_transformerblock_pb_kernel(tc, q_rot, k_rot, v, mask, wo, x, out):
         qT = fixed.tile([P, H, S], BF16)
         e_tiles = [fixed.tile([P, S], BF16, name="e%d" % n) for n in range(E_TILES)]
         e_filled = [S] * E_TILES
-        maskT = {i: fixed.tile([P, i + 1, P], F32, name="maskT%d" % i) for i in TENSOR_MASK}
+        maskT = {i: fixed.tile([P, i + 1, P], F32, name="maskT%d" % i) for i in TENSOR_MASK_TILES}
         rawmax = fixed.tile([P, STEPS], F32)
         negmax = fixed.tile([P, STEPS], F32)
         negmax_v = fixed.tile([P, STEPS], F32)
@@ -164,14 +167,16 @@ def tile_transformerblock_pb_kernel(tc, q_rot, k_rot, v, mask, wo, x, out):
                 load_wo(2)
                 load_vp()
         load_wo(3)
-        nc.sync.dma_start(out=x_sb[:], in_=x2.rearrange("(i p) d -> p i d", p=P))
 
-        nc.gpsimd.memset(vp_half[:], 0)
+        def load_x(i):
+            nc.sync.dma_start(out=x_sb[:, i, :], in_=x2[i * P : (i + 1) * P, :])
+
 
         warm = fixed.tile([P, BANK], BF16)
         nc.vector.memset(warm[:], 0.0)
         make_identity(nc, ident_bf[:])
         make_identity(nc, ident_f32[:])
+        nc.gpsimd.memset(vp_half[:], 0)
 
         def k_job(kv):
             blocks = [k_raw[:, j, kv * HD : (kv + 1) * HD] for j in range(TILES)]
@@ -190,7 +195,7 @@ def tile_transformerblock_pb_kernel(tc, q_rot, k_rot, v, mask, wo, x, out):
         for g in range(1, GROUPS):
             jobs.extend([q_job(first, g), k_job(2 * g), k_job(2 * g + 1)])
         for i in TILE_ORDER[1:]:
-            if i in TENSOR_MASK:
+            if i in TENSOR_MASK_TILES:
                 jobs.append(mask_job(i))
             jobs.extend([q_job(i, g) for g in range(GROUPS)])
 
@@ -231,16 +236,16 @@ def tile_transformerblock_pb_kernel(tc, q_rot, k_rot, v, mask, wo, x, out):
             per_bank = BANK // keys_of(i)
             for a in range(0, GROUP, per_bank):
                 bank_at_step[r * GROUP + a] = len(banks)
-                banks.append((i, (r % GROUPS) * GROUP + a, per_bank))
+                banks.append((i, (r % GROUPS) * GROUP + a, per_bank, r < VECTOR_MASK_ROUND))
         score_tiles = {}
         head_scores = {}
 
         def issue_scores(b):
-            i, h0, per_bank = banks[b]
+            i, h0, per_bank, on_tensor = banks[b]
             keys = keys_of(i)
             scores = ps_scores.tile([P, BANK], F32, name="scores")
             for a in range(per_bank):
-                for j in range(i + 1 if i in TENSOR_MASK else 0):
+                for j in range(i + 1 if on_tensor else 0):
                     nc.tensor.matmul(
                         scores[:, a * keys + j * P : a * keys + (j + 1) * P],
                         lhsT=maskT[i][:, j, :],
@@ -254,14 +259,14 @@ def tile_transformerblock_pb_kernel(tc, q_rot, k_rot, v, mask, wo, x, out):
                     scores[:, a * keys : (a + 1) * keys],
                     lhsT=qT[:, h0 + a, i * P : (i + 1) * P],
                     rhs=kT[:, (h0 + a) // 2, 0:keys],
-                    start=(i not in TENSOR_MASK),
-                    stop=(i not in TENSOR_MASK or a == per_bank - 1),
+                    start=(not on_tensor),
+                    stop=(not on_tensor or a == per_bank - 1),
                 )
             score_tiles[b] = scores
 
         def add_mask(step):
             b = bank_at_step[step]
-            i, h0, per_bank = banks[b]
+            i, h0, per_bank, on_tensor = banks[b]
             keys = keys_of(i)
             masked = work.tile([P, BANK], F32, name="masked", bufs=3)
             nc.vector.scalar_tensor_tensor(
@@ -276,25 +281,26 @@ def tile_transformerblock_pb_kernel(tc, q_rot, k_rot, v, mask, wo, x, out):
 
         def row_max(step):
             b = bank_at_step[step]
-            i, h0, per_bank = banks[b]
+            i, h0, per_bank, on_tensor = banks[b]
             keys = keys_of(i)
             cols = slice(step, step + per_bank)
             nc.vector.tensor_reduce(
-                out=(rawmax if i in TENSOR_MASK else negmax_v)[:, cols],
+                out=(rawmax if on_tensor else negmax_v)[:, cols],
                 in_=score_tiles[b][:, 0 : per_bank * keys].rearrange("p (a n) -> p a n", a=per_bank),
                 axis=mybir.AxisListType.X,
                 op=ALU.max,
                 negate=True,
             )
-            if i in TENSOR_MASK:
-                nc.gpsimd.tensor_scalar(
-                    out=negmax[:, cols], in0=rawmax[:, cols], scalar1=SCALE, scalar2=None, op0=ALU.mult
-                )
             for a in range(per_bank):
                 head_scores[step + a] = score_tiles[b][:, a * keys : (a + 1) * keys]
 
+        def scale_max(step):
+            cols = slice(step, step + banks[bank_at_step[step]][2])
+            nc.scalar.activation(out=negmax[:, cols], in_=rawmax[:, cols], func=ACT.Copy, scale=SCALE)
+
         def exponentials(step):
             i = tile_of_round(step // GROUP)
+            on_tensor = step // GROUP < VECTOR_MASK_ROUND
             keys = keys_of(i)
             if i in PAIRED:
                 n = step // 2 % E_TILES
@@ -314,8 +320,8 @@ def tile_transformerblock_pb_kernel(tc, q_rot, k_rot, v, mask, wo, x, out):
                 out=dst,
                 in_=src,
                 func=ACT.Exp,
-                bias=(negmax if i in TENSOR_MASK else negmax_v)[:, step : step + 1],
-                scale=SCALE if i in TENSOR_MASK else 1.0,
+                bias=(negmax if on_tensor else negmax_v)[:, step : step + 1],
+                scale=SCALE if on_tensor else 1.0,
                 accum_out=rowsum[:, step : step + 1],
             )
 
@@ -503,12 +509,15 @@ def tile_transformerblock_pb_kernel(tc, q_rot, k_rot, v, mask, wo, x, out):
                 residual_steps.setdefault(step + RESIDUAL_LAG, []).append((i, n))
 
         for i, (first_round, per_round) in PROJECT_PLAN.items():
-            for n in range(BLOCKS):
+            for n in range(BLOCKS - (KEPT_BACK if i == TILE_ORDER[-2] else 0)):
                 plan((first_round + n // per_round) * GROUP + HEADS % GROUP, i, n, whole)
         o_done = (ROUNDS - 1) * GROUP + O_QUANT
         for n in range(BLOCKS):
             plan(o_done - 3 + n, TILE_ORDER[-1], n, whole[:-1])
+        for n in range(BLOCKS):
             plan(o_done + 1, TILE_ORDER[-1], n, whole[-1:])
+        for n in range(BLOCKS - KEPT_BACK, BLOCKS):
+            plan(o_done + 1, TILE_ORDER[-2], n, whole)
         last_step = max(residual_steps)
 
         def item_at(step):
@@ -524,7 +533,7 @@ def tile_transformerblock_pb_kernel(tc, q_rot, k_rot, v, mask, wo, x, out):
 
         issue_at_step = {}
         for first_head, b in bank_at_step.items():
-            early = AHEAD if banks[b][0] in TENSOR_MASK else AHEAD + MASK_LEAD
+            early = AHEAD if banks[b][3] else AHEAD + MASK_LEAD
             issue_at_step.setdefault(first_head - early, []).append(b)
         for b in issue_at_step[-AHEAD]:
             issue_scores(b)
@@ -533,10 +542,10 @@ def tile_transformerblock_pb_kernel(tc, q_rot, k_rot, v, mask, wo, x, out):
             item = item_at(step)
 
             ahead = step + MASK_LEAD
-            if ahead in bank_at_step and banks[bank_at_step[ahead]][0] not in TENSOR_MASK:
+            if ahead in bank_at_step and not banks[bank_at_step[ahead]][3]:
                 add_mask(ahead)
                 row_max(ahead)
-            if step in bank_at_step and banks[bank_at_step[step]][0] in TENSOR_MASK:
+            if step in bank_at_step and banks[bank_at_step[step]][3]:
                 row_max(step)
             if 0 <= step - 1 < STEPS:
                 exponentials(step - 1)
@@ -549,6 +558,8 @@ def tile_transformerblock_pb_kernel(tc, q_rot, k_rot, v, mask, wo, x, out):
                 normalise(r)
             for r in rounds_at(step, O_GATHER):
                 gather_o(r)
+            if step in bank_at_step and banks[bank_at_step[step]][3]:
+                scale_max(step)
 
             if step - 1 in job_at_step:
                 finish_job(job_at_step[step - 1], job_flips[step - 1], step < SCALAR_JOBS and step % 2 == 0)
@@ -558,9 +569,9 @@ def tile_transformerblock_pb_kernel(tc, q_rot, k_rot, v, mask, wo, x, out):
                 quantise_o(r)
             for n in range(V_PARTS):
                 if step == V_STEP + n // 2:
-                    interleave_v(0, n, nc.vector if n % 2 == 0 else nc.gpsimd)
+                    interleave_v(0, n, nc.vector)
                 if step == VP_STEP + 2 * n:
-                    interleave_v(1, n, nc.gpsimd)
+                    interleave_v(1, n, nc.vector)
             if step == V_STEP + V_PARTS // 2:
                 quantise_v(0)
             if step == VP_STEP + 2 * V_PARTS:
@@ -588,6 +599,8 @@ def tile_transformerblock_pb_kernel(tc, q_rot, k_rot, v, mask, wo, x, out):
                 flip_wo(item)
                 if item % GROUPS == GROUPS - 1 and item // GROUPS + WO_BUFS < WO_PAIRS:
                     load_wo(item // GROUPS + WO_BUFS)
+            if step >= X_STEP and (step - X_STEP) % GROUP == 0 and (step - X_STEP) // GROUP < TILES:
+                load_x(TILE_ORDER[(step - X_STEP) // GROUP])
             for r in rounds_at(step, HEADS):
                 heads_matmul(r)
             for block in project_steps.get(step, ()):

@@ -38,17 +38,18 @@ WO_BUFS = 4
 TILE_ORDER = (3, 2, 1, 0)
 SCORE_BANKS = 3
 RING_BANKS = 5
-V_STEP = 4
-VP_STEP = 12
+V_STEP = 6
+VP_STEP = 20
 PAIRED = (1, 0)
 V_PARTS = 8
+V_PER_STEP = 3
 VECTOR_WO_FROM = 8
 SCALAR_JOBS = 8
-WO_STEP = 2
+WO_STEP = 3
 WO_QUANT_LAG = 3
-VECTOR_WO = 3
+VECTOR_WO = 4
 RESIDUAL_LAG = 2
-X_STEP = 22
+X_STEP = 28
 KEPT_BACK = 2
 AHEAD = 1
 MASK_LEAD = 2
@@ -60,11 +61,11 @@ NORMALISE = 10
 O_FLIP = 12
 O_GATHER = 13
 O_QUANT = 14
-VECTOR_MASK_ROUND = 10
+VECTOR_MASK_ROUND = 12
 WO_SPACING = 8
 WO_PER = 7
 PROJECT_PLAN = {3: (8, 1), 2: (12, 1), 1: (16, 2)}
-WARM_MATMULS = 5
+WARM_MATMULS = 3
 HEAD_JOBS = 3
 DENSE_JOBS = 10
 TENSOR_MASK_TILES = TILE_ORDER[: -(-VECTOR_MASK_ROUND // GROUPS)]
@@ -96,7 +97,7 @@ def tile_transformerblock_pb_kernel(tc, q_rot, k_rot, v, mask, wo, x, out):
         k_raw = fixed.tile([P, TILES, KV * HD], BF16)
         q_raw = [fixed.tile([P, NQ], BF16, name="q_raw%d" % i) for i in range(TILES)]
         mask_sb = [fixed.tile([P, S], BF16, name="mask%d" % i) for i in range(TILES)]
-        x_sb = fixed.tile([P, TILES, D], BF16)
+        x_rows = {}
         ident_bf = fixed.tile([P, P], BF16)
         ident_f32 = fixed.tile([P, P], F32)
         kT = fixed.tile([P, KV, S], BF16)
@@ -104,9 +105,7 @@ def tile_transformerblock_pb_kernel(tc, q_rot, k_rot, v, mask, wo, x, out):
         e_tiles = [fixed.tile([P, S], BF16, name="e%d" % n) for n in range(E_TILES)]
         e_filled = [S] * E_TILES
         maskT = {i: fixed.tile([P, i + 1, P], F32, name="maskT%d" % i) for i in TENSOR_MASK_TILES}
-        rawmax = fixed.tile([P, STEPS], F32)
         negmax = fixed.tile([P, STEPS], F32)
-        negmax_v = fixed.tile([P, STEPS], F32)
         rowsum = fixed.tile([P, STEPS], F32)
         rinv = fixed.tile([P, STEPS], F32)
         v_codes = fixed.tile([P, KV * HD], U32, align_bytes=64)
@@ -141,35 +140,40 @@ def tile_transformerblock_pb_kernel(tc, q_rot, k_rot, v, mask, wo, x, out):
             nc.sync.dma_start(out=mask_sb[i][:], in_=mask[i * P : (i + 1) * P, :])
 
         def load_vp():
-            v_raw[1] = fixed.tile([P, 2, 2, KV * HD], BF16, name="v_raw")
+            v_raw[1] = fixed.tile([P, 2, 2, KV * HD], BF16, name="v_raw1")
             for h in range(2):
                 nc.sync.dma_start(
                     out=v_raw[1][h * HALF : (h + 1) * HALF], in_=v2[0 : 2 * P, :].rearrange("(u p e) c -> p u e c", u=2, e=2)
                 )
 
-        first = TILE_ORDER[0]
+        def load_v():
+            v_raw[0] = fixed.tile([P, 2, 2, KV * HD], BF16, name="v_raw0")
+            nc.sync.dma_start(out=v_raw[0][:], in_=v2.rearrange("(u p e) c -> p u e c", u=2, e=2))
+
+        v_raw = {}
+        first, second, third, fourth = TILE_ORDER
         load_mask(first)
         load_k(0, 2)
         load_q(first, 0, GROUP)
         load_q(first, GROUP, GROUP)
         load_k(2, 2)
-        load_k(4, KV - 4)
-        load_q(first, 2 * GROUP, H - 2 * GROUP)
+        load_k(4, 4)
+        load_q(first, 2 * GROUP, 2 * GROUP)
         load_wo(0)
-        v_raw = {}
-        v_raw[0] = fixed.tile([P, 2, 2, KV * HD], BF16, name="v_raw")
-        nc.sync.dma_start(out=v_raw[0][:], in_=v2.rearrange("(u p e) c -> p u e c", u=2, e=2))
+        load_v()
         load_wo(1)
-        for i in TILE_ORDER[1:]:
+        load_mask(second)
+        load_q(second, 0, H)
+        load_wo(2)
+        load_wo(3)
+        load_vp()
+        for i in (third, fourth):
             load_mask(i)
             load_q(i, 0, H)
-            if i == TILE_ORDER[1]:
-                load_wo(2)
-                load_vp()
-        load_wo(3)
 
         def load_x(i):
-            nc.sync.dma_start(out=x_sb[:, i, :], in_=x2[i * P : (i + 1) * P, :])
+            x_rows[i] = fixed.tile([P, D], BF16, name="q_raw%d" % i)
+            nc.sync.dma_start(out=x_rows[i][:], in_=x2[i * P : (i + 1) * P, :])
 
 
         warm = fixed.tile([P, BANK], BF16)
@@ -284,19 +288,28 @@ def tile_transformerblock_pb_kernel(tc, q_rot, k_rot, v, mask, wo, x, out):
             i, h0, per_bank, on_tensor = banks[b]
             keys = keys_of(i)
             cols = slice(step, step + per_bank)
-            nc.vector.tensor_reduce(
-                out=(rawmax if on_tensor else negmax_v)[:, cols],
-                in_=score_tiles[b][:, 0 : per_bank * keys].rearrange("p (a n) -> p a n", a=per_bank),
-                axis=mybir.AxisListType.X,
-                op=ALU.max,
-                negate=True,
-            )
+            if on_tensor:
+                for a in range(per_bank):
+                    unused = work.tile([P, BANK], F32, name="unused")
+                    nc.vector.tensor_scalar(
+                        out=unused[:, 0:keys],
+                        in0=score_tiles[b][:, a * keys : (a + 1) * keys],
+                        scalar1=-SCALE,
+                        scalar2=None,
+                        op0=ALU.mult,
+                        op1=ALU.min,
+                        accum_out=negmax[:, step + a : step + a + 1],
+                    )
+            else:
+                nc.vector.tensor_reduce(
+                    out=negmax[:, cols],
+                    in_=score_tiles[b][:, 0 : per_bank * keys].rearrange("p (a n) -> p a n", a=per_bank),
+                    axis=mybir.AxisListType.X,
+                    op=ALU.max,
+                    negate=True,
+                )
             for a in range(per_bank):
                 head_scores[step + a] = score_tiles[b][:, a * keys : (a + 1) * keys]
-
-        def scale_max(step):
-            cols = slice(step, step + banks[bank_at_step[step]][2])
-            nc.scalar.activation(out=negmax[:, cols], in_=rawmax[:, cols], func=ACT.Copy, scale=SCALE)
 
         def exponentials(step):
             i = tile_of_round(step // GROUP)
@@ -320,7 +333,7 @@ def tile_transformerblock_pb_kernel(tc, q_rot, k_rot, v, mask, wo, x, out):
                 out=dst,
                 in_=src,
                 func=ACT.Exp,
-                bias=(negmax if on_tensor else negmax_v)[:, step : step + 1],
+                bias=negmax[:, step : step + 1],
                 scale=SCALE if on_tensor else 1.0,
                 accum_out=rowsum[:, step : step + 1],
             )
@@ -417,18 +430,14 @@ def tile_transformerblock_pb_kernel(tc, q_rot, k_rot, v, mask, wo, x, out):
 
         v_grouped = {}
 
-        def interleave_v(which, n, engine):
+        def interleave_v(which, n):
             if n == 0:
                 v_grouped[which] = fixed.tile([P, KV * HD, 4], BF16, name="v_grouped", align_bytes=64)
             width = KV * HD // V_PARTS
             part = slice(n * width, (n + 1) * width)
-            engine.tensor_scalar(
-                out=v_grouped[which][:, part, :],
-                in0=v_raw[which][:, :, :, part].rearrange("p u e c -> p c (u e)"),
-                scalar1=1.0,
-                scalar2=0.0,
-                op0=ALU.mult,
-                op1=ALU.add,
+            nc.vector.tensor_copy(
+                out=v_grouped[which][:, part, :].rearrange("p (c i) t -> p c t i", i=4),
+                in_=v_raw[which][:, :, :, part].rearrange("p u e (c i) -> p c (u e) i", i=4),
             )
 
         def quantise_v(which):
@@ -495,8 +504,8 @@ def tile_transformerblock_pb_kernel(tc, q_rot, k_rot, v, mask, wo, x, out):
         def add_residual(i, n):
             rows = slice(i * P, (i + 1) * P)
             cols = slice(n * BANK, (n + 1) * BANK)
-            result = work.tile([P, BANK], F32, name="result", bufs=4)
-            nc.vector.tensor_tensor(out=result[:], in0=sums[(i, n)][:], in1=x_sb[:, i, cols], op=ALU.add)
+            result = work.tile([P, BANK], F32, name="result", bufs=6)
+            nc.vector.tensor_tensor(out=result[:], in0=sums[(i, n)][:], in1=x_rows[i][:, cols], op=ALU.add)
             nc.sync.dma_start(out=out2[rows, cols], in_=result[:])
 
         project_steps = {}
@@ -558,8 +567,6 @@ def tile_transformerblock_pb_kernel(tc, q_rot, k_rot, v, mask, wo, x, out):
                 normalise(r)
             for r in rounds_at(step, O_GATHER):
                 gather_o(r)
-            if step in bank_at_step and banks[bank_at_step[step]][3]:
-                scale_max(step)
 
             if step - 1 in job_at_step:
                 finish_job(job_at_step[step - 1], job_flips[step - 1], step < SCALAR_JOBS and step % 2 == 0)
@@ -568,11 +575,11 @@ def tile_transformerblock_pb_kernel(tc, q_rot, k_rot, v, mask, wo, x, out):
             for r in rounds_at(step, O_QUANT):
                 quantise_o(r)
             for n in range(V_PARTS):
-                if step == V_STEP + n // 2:
-                    interleave_v(0, n, nc.vector)
+                if step == V_STEP + n // V_PER_STEP:
+                    interleave_v(0, n)
                 if step == VP_STEP + 2 * n:
-                    interleave_v(1, n, nc.vector)
-            if step == V_STEP + V_PARTS // 2:
+                    interleave_v(1, n)
+            if step == V_STEP + -(-V_PARTS // V_PER_STEP):
                 quantise_v(0)
             if step == VP_STEP + 2 * V_PARTS:
                 quantise_v(1)

@@ -38,14 +38,14 @@ WO_BUFS = 4
 TILE_ORDER = (3, 2, 1, 0)
 SCORE_BANKS = 3
 RING_BANKS = 5
-V_STEP = 6
+V_STEP = 4
 VP_STEP = 20
 PAIRED = (1, 0)
 V_PARTS = 8
-V_PER_STEP = 3
+V_PER_STEP = 2
 VECTOR_WO_FROM = 8
 SCALAR_JOBS = 8
-WO_STEP = 3
+WO_STEP = 5
 WO_QUANT_LAG = 3
 VECTOR_WO = 4
 RESIDUAL_LAG = 2
@@ -64,7 +64,7 @@ O_QUANT = 14
 VECTOR_MASK_ROUND = 12
 WO_SPACING = 8
 WO_PER = 7
-PROJECT_PLAN = {3: (8, 1), 2: (12, 1), 1: (16, 2)}
+PROJECT_PLAN = {3: (8, 9, 10, 11), 2: (12, 13, 14, 15), 1: (16, 16, 17, 17)}
 WARM_MATMULS = 3
 HEAD_JOBS = 3
 DENSE_JOBS = 10
@@ -106,6 +106,8 @@ def tile_transformerblock_pb_kernel(tc, q_rot, k_rot, v, mask, wo, x, out):
         e_filled = [S] * E_TILES
         maskT = {i: fixed.tile([P, i + 1, P], F32, name="maskT%d" % i) for i in TENSOR_MASK_TILES}
         negmax = fixed.tile([P, STEPS], F32)
+        rawmax = fixed.tile([P, STEPS], F32)
+        scaledmax = fixed.tile([P, STEPS], F32)
         rowsum = fixed.tile([P, STEPS], F32)
         rinv = fixed.tile([P, STEPS], F32)
         v_codes = fixed.tile([P, KV * HD], U32, align_bytes=64)
@@ -157,10 +159,10 @@ def tile_transformerblock_pb_kernel(tc, q_rot, k_rot, v, mask, wo, x, out):
         load_q(first, 0, GROUP)
         load_q(first, GROUP, GROUP)
         load_k(2, 2)
+        load_v()
         load_k(4, 4)
         load_q(first, 2 * GROUP, 2 * GROUP)
         load_wo(0)
-        load_v()
         load_wo(1)
         load_mask(second)
         load_q(second, 0, H)
@@ -288,28 +290,19 @@ def tile_transformerblock_pb_kernel(tc, q_rot, k_rot, v, mask, wo, x, out):
             i, h0, per_bank, on_tensor = banks[b]
             keys = keys_of(i)
             cols = slice(step, step + per_bank)
-            if on_tensor:
-                for a in range(per_bank):
-                    unused = work.tile([P, BANK], F32, name="unused")
-                    nc.vector.tensor_scalar(
-                        out=unused[:, 0:keys],
-                        in0=score_tiles[b][:, a * keys : (a + 1) * keys],
-                        scalar1=-SCALE,
-                        scalar2=None,
-                        op0=ALU.mult,
-                        op1=ALU.min,
-                        accum_out=negmax[:, step + a : step + a + 1],
-                    )
-            else:
-                nc.vector.tensor_reduce(
-                    out=negmax[:, cols],
-                    in_=score_tiles[b][:, 0 : per_bank * keys].rearrange("p (a n) -> p a n", a=per_bank),
-                    axis=mybir.AxisListType.X,
-                    op=ALU.max,
-                    negate=True,
-                )
+            nc.vector.tensor_reduce(
+                out=(rawmax if on_tensor else negmax)[:, cols],
+                in_=score_tiles[b][:, 0 : per_bank * keys].rearrange("p (a n) -> p a n", a=per_bank),
+                axis=mybir.AxisListType.X,
+                op=ALU.max,
+                negate=True,
+            )
             for a in range(per_bank):
                 head_scores[step + a] = score_tiles[b][:, a * keys : (a + 1) * keys]
+
+        def scale_max(step):
+            cols = slice(step, step + banks[bank_at_step[step]][2])
+            nc.scalar.activation(out=scaledmax[:, cols], in_=rawmax[:, cols], func=ACT.Copy, scale=SCALE)
 
         def exponentials(step):
             i = tile_of_round(step // GROUP)
@@ -333,7 +326,7 @@ def tile_transformerblock_pb_kernel(tc, q_rot, k_rot, v, mask, wo, x, out):
                 out=dst,
                 in_=src,
                 func=ACT.Exp,
-                bias=negmax[:, step : step + 1],
+                bias=(scaledmax if on_tensor else negmax)[:, step : step + 1],
                 scale=SCALE if on_tensor else 1.0,
                 accum_out=rowsum[:, step : step + 1],
             )
@@ -430,15 +423,17 @@ def tile_transformerblock_pb_kernel(tc, q_rot, k_rot, v, mask, wo, x, out):
 
         v_grouped = {}
 
-        def interleave_v(which, n):
+        def interleave_v(which, n, on_gpsimd):
             if n == 0:
                 v_grouped[which] = fixed.tile([P, KV * HD, 4], BF16, name="v_grouped", align_bytes=64)
             width = KV * HD // V_PARTS
             part = slice(n * width, (n + 1) * width)
-            nc.vector.tensor_copy(
-                out=v_grouped[which][:, part, :].rearrange("p (c i) t -> p c t i", i=4),
-                in_=v_raw[which][:, :, :, part].rearrange("p u e (c i) -> p c (u e) i", i=4),
-            )
+            dst = v_grouped[which][:, part, :].rearrange("p (c i) t -> p c t i", i=4)
+            src = v_raw[which][:, :, :, part].rearrange("p u e (c i) -> p c (u e) i", i=4)
+            if on_gpsimd:
+                nc.gpsimd.tensor_scalar(out=dst, in0=src, scalar1=1.0, scalar2=0.0, op0=ALU.mult, op1=ALU.add)
+            else:
+                nc.vector.tensor_copy(out=dst, in_=src)
 
         def quantise_v(which):
             codes, scales = ((v_codes, v_scales), (vp_codes, vp_scales))[which]
@@ -449,7 +444,7 @@ def tile_transformerblock_pb_kernel(tc, q_rot, k_rot, v, mask, wo, x, out):
         def spread_vp():
             for h in range(2):
                 rows = slice(h * HALF, (h + 1) * HALF)
-                nc.vector.tensor_copy(out=vp_half[rows, h, :].bitcast(I32), in_=vp_codes[rows, :].bitcast(I32))
+                nc.gpsimd.tensor_copy(out=vp_half[rows, h, :], in_=vp_codes[rows, :])
 
         wo_flips = {}
         wo_grouped = {}
@@ -517,9 +512,9 @@ def tile_transformerblock_pb_kernel(tc, q_rot, k_rot, v, mask, wo, x, out):
             if groups[-1] == GROUPS - 1:
                 residual_steps.setdefault(step + RESIDUAL_LAG, []).append((i, n))
 
-        for i, (first_round, per_round) in PROJECT_PLAN.items():
+        for i, rounds in PROJECT_PLAN.items():
             for n in range(BLOCKS - (KEPT_BACK if i == TILE_ORDER[-2] else 0)):
-                plan((first_round + n // per_round) * GROUP + HEADS % GROUP, i, n, whole)
+                plan(rounds[n] * GROUP + HEADS % GROUP, i, n, whole)
         o_done = (ROUNDS - 1) * GROUP + O_QUANT
         for n in range(BLOCKS):
             plan(o_done - 3 + n, TILE_ORDER[-1], n, whole[:-1])
@@ -565,6 +560,8 @@ def tile_transformerblock_pb_kernel(tc, q_rot, k_rot, v, mask, wo, x, out):
                         gather_e(r, half)
             for r in rounds_at(step, NORMALISE):
                 normalise(r)
+            if step in bank_at_step and banks[bank_at_step[step]][3]:
+                scale_max(step)
             for r in rounds_at(step, O_GATHER):
                 gather_o(r)
 
@@ -576,9 +573,9 @@ def tile_transformerblock_pb_kernel(tc, q_rot, k_rot, v, mask, wo, x, out):
                 quantise_o(r)
             for n in range(V_PARTS):
                 if step == V_STEP + n // V_PER_STEP:
-                    interleave_v(0, n)
+                    interleave_v(0, n, False)
                 if step == VP_STEP + 2 * n:
-                    interleave_v(1, n)
+                    interleave_v(1, n, True)
             if step == V_STEP + -(-V_PARTS // V_PER_STEP):
                 quantise_v(0)
             if step == VP_STEP + 2 * V_PARTS:

@@ -38,8 +38,8 @@ WO_BUFS = 4
 TILE_ORDER = (3, 2, 1, 0)
 SCORE_BANKS = 3
 RING_BANKS = 5
-V_STEP = 4
-VP_STEP = 20
+V_STEP = 3
+VP_STEP = 16
 PAIRED = (1, 0)
 V_PARTS = 8
 V_PER_STEP = 2

@@ -38,36 +38,32 @@ WO_BUFS = 4
 TILE_ORDER = (3, 2, 1, 0)
 SCORE_BANKS = 3
 RING_BANKS = 5
-V_STEP = 3
-VP_STEP = 16
-PAIRED = (1, 0)
 V_PARTS = 8
-V_PER_STEP = 2
-VECTOR_WO_FROM = 8
-SCALAR_JOBS = 8
-WO_STEP = 5
-WO_QUANT_LAG = 3
+V_QUARTERS = 4
+V_STEP = 4
+VP_STEP = 22
+PAIRED = (1, 0)
 VECTOR_WO = 4
-RESIDUAL_LAG = 2
+WO_STEP = 7
 X_STEP = 28
-KEPT_BACK = 2
-AHEAD = 1
-MASK_LEAD = 2
-E_FLIP = (3, 5)
-E_GATHER = (4, 6)
-E_QUANT = 7
-HEADS = 9
-NORMALISE = 10
-O_FLIP = 12
-O_GATHER = 13
-O_QUANT = 14
+X_LAG = 3
+KEPT_BACK = 1
+JOB_LEAD = 5
+DENSE_JOBS = 10
 VECTOR_MASK_ROUND = 12
-WO_SPACING = 8
-WO_PER = 7
-PROJECT_PLAN = {3: (8, 9, 10, 11), 2: (12, 13, 14, 15), 1: (16, 16, 17, 17)}
 WARM_MATMULS = 3
 HEAD_JOBS = 3
-DENSE_JOBS = 10
+E_FLIP = (3, 5)
+E_GATHER = (4, 6)
+E_QUANT = 8
+HEADS = 10
+NORMALISE = 11
+O_FLIP = 12
+O_GATHER = 13
+O_QUANT = 15
+WO_QUANT_LAG = 2
+PROJECT = 3
+MASK_LEAD = 2
 TENSOR_MASK_TILES = TILE_ORDER[: -(-VECTOR_MASK_ROUND // GROUPS)]
 
 FLOPS = 2 * (2 * H * S * S * HD) + 2 * S * D * NQ
@@ -197,13 +193,17 @@ def tile_transformerblock_pb_kernel(tc, q_rot, k_rot, v, mask, wo, x, out):
             blocks = [mask_sb[i][:, j * P : (j + 1) * P] for j in range(i + 1)]
             return (blocks, maskT[i][:], ROOT)
 
-        jobs = [mask_job(first), k_job(0), q_job(first, 0), k_job(1)]
-        for g in range(1, GROUPS):
-            jobs.extend([q_job(first, g), k_job(2 * g), k_job(2 * g + 1)])
-        for i in TILE_ORDER[1:]:
-            if i in TENSOR_MASK_TILES:
-                jobs.append(mask_job(i))
-            jobs.extend([q_job(i, g) for g in range(GROUPS)])
+        jobs = []
+        for r in range(ROUNDS):
+            i, g = tile_of_round(r), r % GROUPS
+            needed = r * GROUP
+            if g == 0 and i in TENSOR_MASK_TILES:
+                jobs.append((needed, mask_job(i)))
+            if i == first:
+                jobs.append((needed, k_job(2 * g)))
+            jobs.append((needed, q_job(i, g)))
+            if i == first:
+                jobs.append((needed + 2, k_job(2 * g + 1)))
 
         def flip_job(job):
             flip = ps_ring.tile([P, 4, P], BF16, name="ring")
@@ -229,11 +229,22 @@ def tile_transformerblock_pb_kernel(tc, q_rot, k_rot, v, mask, wo, x, out):
             nc.tensor.matmul(warm_sums[:], lhsT=warm[:, 0:P], rhs=warm[:], start=True, stop=True)
 
         for n in range(HEAD_JOBS):
-            finish_job(jobs[n], flip_job(jobs[n]), n % 2 == 0)
+            finish_job(jobs[n][1], flip_job(jobs[n][1]), n % 2 == 0)
+        latest = []
+        limit = STEPS
+        for needed, job in reversed(jobs[HEAD_JOBS:]):
+            limit = min(limit - (1 if len(jobs) - len(latest) <= HEAD_JOBS + DENSE_JOBS else 2), needed - JOB_LEAD)
+            latest.append((limit, job))
         job_at_step = {}
-        for n in range(HEAD_JOBS, len(jobs)):
-            late = n - HEAD_JOBS - DENSE_JOBS
-            job_at_step[n - HEAD_JOBS if late < 0 else DENSE_JOBS + 1 + 2 * late] = jobs[n]
+        free = 0
+        for limit, job in reversed(latest):
+            free = max(free, limit)
+            job_at_step[free] = job
+            free += 1
+        x_at_step = {}
+        for n, i in enumerate(TILE_ORDER):
+            x_step = max(X_STEP + n * GROUP, (n + 1) * GROUPS * GROUP - GROUP - JOB_LEAD + X_LAG)
+            x_at_step.setdefault(x_step, []).append(i)
 
         banks = []
         bank_at_step = {}
@@ -423,22 +434,23 @@ def tile_transformerblock_pb_kernel(tc, q_rot, k_rot, v, mask, wo, x, out):
 
         v_grouped = {}
 
-        def interleave_v(which, n, on_gpsimd):
+        def interleave_v(which, n):
             if n == 0:
                 v_grouped[which] = fixed.tile([P, KV * HD, 4], BF16, name="v_grouped", align_bytes=64)
             width = KV * HD // V_PARTS
             part = slice(n * width, (n + 1) * width)
             dst = v_grouped[which][:, part, :].rearrange("p (c i) t -> p c t i", i=4)
             src = v_raw[which][:, :, :, part].rearrange("p u e (c i) -> p c (u e) i", i=4)
-            if on_gpsimd:
-                nc.gpsimd.tensor_scalar(out=dst, in0=src, scalar1=1.0, scalar2=0.0, op0=ALU.mult, op1=ALU.add)
-            else:
-                nc.vector.tensor_copy(out=dst, in_=src)
+            nc.gpsimd.tensor_scalar(out=dst, in0=src, scalar1=1.0, scalar2=0.0, op0=ALU.mult, op1=ALU.add)
 
-        def quantise_v(which):
+        def quantise_v(which, part, parts):
             codes, scales = ((v_codes, v_scales), (vp_codes, vp_scales))[which]
+            width = KV * HD // parts
+            cols = slice(part * width, (part + 1) * width)
             nc.vector.quantize_mx(
-                out=codes[:].bitcast(FP8X4), scales=scales[:], in_=v_grouped[which][:].rearrange("p c t -> p (c t)")
+                out=codes[:, cols].bitcast(FP8X4),
+                scales=scales[:, cols],
+                in_=v_grouped[which][:, cols, :].rearrange("p c t -> p (c t)"),
             )
 
         def spread_vp():
@@ -463,7 +475,7 @@ def tile_transformerblock_pb_kernel(tc, q_rot, k_rot, v, mask, wo, x, out):
             wo_grouped[item] = work.tile([P, 4 * 2 * P], BF16, name="wo_grouped", align_bytes=64, bufs=3)
             dst = wo_grouped[item][:].bitcast(F32).rearrange("p (r d u) -> p r d u", r=2, u=2)
             src = wo_flips[item][:].rearrange("p (r u) d -> p r d u", u=2)
-            if item >= VECTOR_WO_FROM and item % VECTOR_WO == VECTOR_WO - 1:
+            if item % VECTOR_WO == VECTOR_WO - 1:
                 nc.vector.tensor_copy(out=dst, in_=src)
             else:
                 nc.scalar.copy(out=dst, in_=src)
@@ -510,102 +522,110 @@ def tile_transformerblock_pb_kernel(tc, q_rot, k_rot, v, mask, wo, x, out):
         def plan(step, i, n, groups):
             project_steps.setdefault(step, []).append((i, n, groups))
             if groups[-1] == GROUPS - 1:
-                residual_steps.setdefault(step + RESIDUAL_LAG, []).append((i, n))
+                residual_steps.setdefault(step + 1, []).append((i, n))
 
-        for i, rounds in PROJECT_PLAN.items():
+        r = 0
+        for i in TILE_ORDER[:-1]:
+            o_ready = GROUP * ((TILE_ORDER.index(i) + 1) * GROUPS - 1) + O_QUANT
             for n in range(BLOCKS - (KEPT_BACK if i == TILE_ORDER[-2] else 0)):
-                plan(rounds[n] * GROUP + HEADS % GROUP, i, n, whole)
+                wo_ready = WO_STEP + (n + 1) * WO_ITEMS // BLOCKS - 1 + WO_QUANT_LAG
+                r = max(r, -(-max(o_ready, wo_ready) // GROUP))
+                plan(min(r, ROUNDS + 1) * GROUP + PROJECT, i, n, whole)
+                r += 1
         o_done = (ROUNDS - 1) * GROUP + O_QUANT
         for n in range(BLOCKS):
-            plan(o_done - 3 + n, TILE_ORDER[-1], n, whole[:-1])
+            plan(o_done - BLOCKS + n, TILE_ORDER[-1], n, whole[:-1])
         for n in range(BLOCKS):
-            plan(o_done + 1, TILE_ORDER[-1], n, whole[-1:])
+            plan(o_done, TILE_ORDER[-1], n, whole[-1:])
         for n in range(BLOCKS - KEPT_BACK, BLOCKS):
-            plan(o_done + 1, TILE_ORDER[-2], n, whole)
+            plan(o_done, TILE_ORDER[-2], n, whole)
         last_step = max(residual_steps)
 
         def item_at(step):
-            t = step - WO_STEP
-            if t < 0 or t % WO_SPACING >= WO_PER:
-                return None
-            item = t // WO_SPACING * WO_PER + t % WO_SPACING
-            return item if item < WO_ITEMS else None
+            item = step - WO_STEP
+            return item if 0 <= item < WO_ITEMS else None
 
         def rounds_at(step, offset):
             r, a = divmod(step - offset, GROUP)
             return [r] if a == 0 and 0 <= r < ROUNDS else []
 
+        def halves_at(step, offsets):
+            pairs = [(r, half) for half in range(2) for r in rounds_at(step, offsets[half])]
+            return [(r, half) for r, half in pairs if half == 1 or tile_of_round(r) not in PAIRED]
+
         issue_at_step = {}
         for first_head, b in bank_at_step.items():
-            early = AHEAD if banks[b][3] else AHEAD + MASK_LEAD
+            early = 1 if banks[b][3] else 1 + MASK_LEAD
             issue_at_step.setdefault(first_head - early, []).append(b)
-        for b in issue_at_step[-AHEAD]:
+        for b in issue_at_step[-1]:
             issue_scores(b)
-        job_flips = {}
         for step in range(last_step + 1):
             item = item_at(step)
-
+            on_tensor = step in bank_at_step and banks[bank_at_step[step]][3]
             ahead = step + MASK_LEAD
+
+            if on_tensor:
+                row_max(step)
             if ahead in bank_at_step and not banks[bank_at_step[ahead]][3]:
                 add_mask(ahead)
                 row_max(ahead)
-            if step in bank_at_step and banks[bank_at_step[step]][3]:
-                row_max(step)
-            if 0 <= step - 1 < STEPS:
-                exponentials(step - 1)
-
-            for half in range(2):
-                for r in rounds_at(step, E_GATHER[half]):
-                    if half == 1 or tile_of_round(r) not in PAIRED:
-                        gather_e(r, half)
-            for r in rounds_at(step, NORMALISE):
-                normalise(r)
-            if step in bank_at_step and banks[bank_at_step[step]][3]:
-                scale_max(step)
-            for r in rounds_at(step, O_GATHER):
-                gather_o(r)
-
-            if step - 1 in job_at_step:
-                finish_job(job_at_step[step - 1], job_flips[step - 1], step < SCALAR_JOBS and step % 2 == 0)
             for r in rounds_at(step, E_QUANT):
                 quantise_e(r)
+            for r in rounds_at(step, NORMALISE):
+                normalise(r)
             for r in rounds_at(step, O_QUANT):
                 quantise_o(r)
-            for n in range(V_PARTS):
-                if step == V_STEP + n // V_PER_STEP:
-                    interleave_v(0, n, False)
-                if step == VP_STEP + 2 * n:
-                    interleave_v(1, n, True)
-            if step == V_STEP + -(-V_PARTS // V_PER_STEP):
-                quantise_v(0)
-            if step == VP_STEP + 2 * V_PARTS:
-                quantise_v(1)
-            if step == VP_STEP + 2 * V_PARTS + 2:
+            quarter, phase = divmod(step - V_STEP, GROUP)
+            if 0 <= quarter < V_QUARTERS:
+                if phase == 0:
+                    interleave_v(0, 2 * quarter)
+                    interleave_v(0, 2 * quarter + 1)
+            if 0 <= step - VP_STEP < V_PARTS:
+                interleave_v(1, step - VP_STEP)
+            elif step == VP_STEP + V_PARTS:
+                quantise_v(1, 0, 1)
+            elif step == VP_STEP + V_PARTS + 2:
                 spread_vp()
-            if item_at(step - 1) is not None:
-                gather_wo(item_at(step - 1))
-            if item_at(step - WO_QUANT_LAG) is not None:
-                quantise_wo(item_at(step - WO_QUANT_LAG))
-            for block in residual_steps.get(step, ()):
-                add_residual(*block)
 
-            for b in issue_at_step.get(step, ()):
-                issue_scores(b)
-            for half in range(2):
-                for r in rounds_at(step, E_FLIP[half]):
-                    if half == 1 or tile_of_round(r) not in PAIRED:
-                        flip_e(r, half)
-            for r in rounds_at(step, O_FLIP):
-                flip_o(r)
             if step in job_at_step:
-                job_flips[step] = flip_job(job_at_step[step])
+                job_flip = flip_job(job_at_step[step])
             if item is not None:
                 flip_wo(item)
                 if item % GROUPS == GROUPS - 1 and item // GROUPS + WO_BUFS < WO_PAIRS:
                     load_wo(item // GROUPS + WO_BUFS)
-            if step >= X_STEP and (step - X_STEP) % GROUP == 0 and (step - X_STEP) // GROUP < TILES:
-                load_x(TILE_ORDER[(step - X_STEP) // GROUP])
+            for b in issue_at_step.get(step, ()):
+                if banks[b][3]:
+                    issue_scores(b)
+            if 0 <= step - 1 < STEPS:
+                exponentials(step - 1)
+            for r, half in halves_at(step, E_FLIP):
+                flip_e(r, half)
+            for r, half in halves_at(step, E_GATHER):
+                gather_e(r, half)
             for r in rounds_at(step, HEADS):
                 heads_matmul(r)
+            for r in rounds_at(step, O_FLIP):
+                flip_o(r)
             for block in project_steps.get(step, ()):
                 project(*block)
+
+            for b in issue_at_step.get(step, ()):
+                if not banks[b][3]:
+                    issue_scores(b)
+
+            if 0 <= quarter < V_QUARTERS and phase == 1:
+                quantise_v(0, quarter, V_QUARTERS)
+            if on_tensor:
+                scale_max(step)
+            for r in rounds_at(step, O_GATHER):
+                gather_o(r)
+            if item_at(step - WO_QUANT_LAG) is not None:
+                quantise_wo(item_at(step - WO_QUANT_LAG))
+            if step in job_at_step:
+                finish_job(job_at_step[step], job_flip, False)
+            if item is not None:
+                gather_wo(item)
+            for block in residual_steps.get(step, ()):
+                add_residual(*block)
+            for i in x_at_step.get(step, ()):
+                load_x(i)

@@ -37,6 +37,7 @@ WO_ITEMS = WO_PAIRS * GROUPS
 WO_BUFS = 4
 TILE_ORDER = (3, 2, 1, 0)
 SCORE_BANKS = 3
+BORROWED = 1
 RING_BANKS = 5
 V_PARTS = 8
 V_QUARTERS = 4
@@ -260,7 +261,10 @@ def tile_transformerblock_pb_kernel(tc, q_rot, k_rot, v, mask, wo, x, out):
         def issue_scores(b):
             i, h0, per_bank, on_tensor = banks[b]
             keys = keys_of(i)
-            scores = ps_scores.tile([P, BANK], F32, name="scores")
+            if b == BORROWED:
+                scores = ps_ring.tile([P, BANK], F32, name="ring")
+            else:
+                scores = ps_scores.tile([P, BANK], F32, name="scores")
             for a in range(per_bank):
                 for j in range(i + 1 if on_tensor else 0):
                     nc.tensor.matmul(
@@ -533,12 +537,14 @@ def tile_transformerblock_pb_kernel(tc, q_rot, k_rot, v, mask, wo, x, out):
                 plan(min(r, ROUNDS + 1) * GROUP + PROJECT, i, n, whole)
                 r += 1
         o_done = (ROUNDS - 1) * GROUP + O_QUANT
-        for n in range(BLOCKS):
+        for n in range(SCORE_BANKS):
             plan(o_done - BLOCKS + n, TILE_ORDER[-1], n, whole[:-1])
-        for n in range(BLOCKS):
+        for n in range(SCORE_BANKS):
             plan(o_done, TILE_ORDER[-1], n, whole[-1:])
         for n in range(BLOCKS - KEPT_BACK, BLOCKS):
             plan(o_done, TILE_ORDER[-2], n, whole)
+        for n in range(SCORE_BANKS, BLOCKS):
+            plan(o_done, TILE_ORDER[-1], n, whole)
         last_step = max(residual_steps)
 
         def item_at(step):
@@ -575,6 +581,8 @@ def tile_transformerblock_pb_kernel(tc, q_rot, k_rot, v, mask, wo, x, out):
                 normalise(r)
             for r in rounds_at(step, O_QUANT):
                 quantise_o(r)
+            if item_at(step - WO_QUANT_LAG) is not None:
+                quantise_wo(item_at(step - WO_QUANT_LAG))
             quarter, phase = divmod(step - V_STEP, GROUP)
             if 0 <= quarter < V_QUARTERS:
                 if phase == 0:
@@ -619,8 +627,6 @@ def tile_transformerblock_pb_kernel(tc, q_rot, k_rot, v, mask, wo, x, out):
                 scale_max(step)
             for r in rounds_at(step, O_GATHER):
                 gather_o(r)
-            if item_at(step - WO_QUANT_LAG) is not None:
-                quantise_wo(item_at(step - WO_QUANT_LAG))
             if step in job_at_step:
                 finish_job(job_at_step[step], job_flip, False)
             if item is not None:

import math
from contextlib import ExitStack

import concourse.mybir as mybir
from concourse.masks import make_identity

BF16 = mybir.dt.bfloat16
F32 = mybir.dt.float32
U32 = mybir.dt.uint32
I32 = mybir.dt.int32
U8 = mybir.dt.uint8
FP8X4 = mybir.dt.float8_e4m3fn_x4
ALU = mybir.AluOpType
ACT = mybir.ActivationFunctionType

P = 128
HALF = P // 2
S = 512
H = 16
KV = 8
HD = 128
D = 2048
NQ = H * HD
TILES = S // P
GROUP = 4
GROUPS = H // GROUP
BANK = 512
BLOCKS = D // BANK
E_TILES = 2 * GROUP
ROOT = math.sqrt(HD)
SCALE = 1.0 / ROOT

ROUNDS = TILES * GROUPS
STEPS = ROUNDS * GROUP
WO_PAIRS = D // (2 * P)
WO_ITEMS = WO_PAIRS * GROUPS
WO_BUFS = 4
TILE_ORDER = (3, 2, 1, 0)
SCORE_BANKS = 3
BORROWED = 1
RING_BANKS = 5
V_PARTS = 8
V_QUARTERS = 4
V_STEP = 4
VP_STEP = 22
PAIRED = (1, 0)
VECTOR_WO = 4
WO_STEP = 7
X_STEP = 28
X_LAG = 3
KEPT_BACK = 1
JOB_LEAD = 5
DENSE_JOBS = 10
VECTOR_MASK_ROUND = 12
WARM_MATMULS = 3
HEAD_JOBS = 3
E_FLIP = (3, 5)
E_GATHER = (4, 6)
E_QUANT = 8
HEADS = 10
NORMALISE = 11
O_FLIP = 12
O_GATHER = 13
O_QUANT = 15
WO_QUANT_LAG = 2
PROJECT = 3
MASK_LEAD = 2
TENSOR_MASK_TILES = TILE_ORDER[: -(-VECTOR_MASK_ROUND // GROUPS)]

FLOPS = 2 * (2 * H * S * S * HD) + 2 * S * D * NQ


def tile_transformerblock_pb_kernel(tc, q_rot, k_rot, v, mask, wo, x, out):
    nc = tc.nc
    q2 = q_rot.rearrange("b s h d -> (b s) (h d)")
    k2 = k_rot.rearrange("b s h d -> (b s) (h d)")
    v2 = v.rearrange("b s h d -> (b s) (h d)")
    x2 = x.rearrange("b s d -> (b s) d")
    out2 = out.rearrange("b s d -> (b s) d")

    with ExitStack() as stack:
        fixed = stack.enter_context(tc.tile_pool(name="fixed", bufs=1))
        work = stack.enter_context(tc.tile_pool(name="work", bufs=2))
        ps_scores = stack.enter_context(tc.psum_pool(name="ps_scores", bufs=SCORE_BANKS))
        ps_ring = stack.enter_context(tc.psum_pool(name="ps_ring", bufs=RING_BANKS))
        stack.enter_context(tc.manual_schedule())

        def tile_of_round(r):
            return TILE_ORDER[r // GROUPS]

        def keys_of(i):
            return (i + 1) * P

        k_raw = fixed.tile([P, TILES, KV * HD], BF16)
        q_raw = [fixed.tile([P, NQ], BF16, name="q_raw%d" % i) for i in range(TILES)]
        mask_sb = [fixed.tile([P, S], BF16, name="mask%d" % i) for i in range(TILES)]
        x_rows = {}
        ident_bf = fixed.tile([P, P], BF16)
        ident_f32 = fixed.tile([P, P], F32)
        kT = fixed.tile([P, KV, S], BF16)
        qT = fixed.tile([P, H, S], BF16)
        e_tiles = [fixed.tile([P, S], BF16, name="e%d" % n) for n in range(E_TILES)]
        e_filled = [S] * E_TILES
        maskT = {i: fixed.tile([P, i + 1, P], F32, name="maskT%d" % i) for i in TENSOR_MASK_TILES}
        negmax = fixed.tile([P, STEPS], F32)
        rawmax = fixed.tile([P, STEPS], F32)
        scaledmax = fixed.tile([P, STEPS], F32)
        rowsum = fixed.tile([P, STEPS], F32)
        rinv = fixed.tile([P, STEPS], F32)
        v_codes = fixed.tile([P, KV * HD], U32, align_bytes=64)
        v_scales = fixed.tile([P, KV * HD], U8, align_bytes=64)
        vp_codes = fixed.tile([P, KV * HD], U32, align_bytes=64)
        vp_scales = fixed.tile([P, KV * HD], U8, align_bytes=64)
        vp_half = fixed.tile([P, 2, KV * HD], U32, align_bytes=64)
        wo_codes = fixed.tile([P, GROUPS, D], U32, align_bytes=64)
        wo_scales = fixed.tile([P, GROUPS, D], U8, align_bytes=64)
        o_codes = fixed.tile([P, GROUPS, S], U32, align_bytes=64)
        o_scales = fixed.tile([P, GROUPS, S], U8, align_bytes=64)

        wo_raw = {}

        def load_wo(pr):
            wo_raw[pr] = work.tile([P, 2, NQ], BF16, name="wo_raw", bufs=WO_BUFS)
            nc.sync.dma_start(
                out=wo_raw[pr][:], in_=wo[pr * 2 * P : (pr + 1) * 2 * P, :].rearrange("(r p) k -> p r k", p=P)
            )

        k_view = k2.rearrange("(j p) c -> p j c", p=P)

        def load_k(kv, count):
            cols = slice(kv * HD, (kv + count) * HD)
            nc.sync.dma_start(out=k_raw[:, :, cols], in_=k_view[:, :, cols])

        def load_q(i, h, count):
            cols = slice(h * HD, (h + count) * HD)
            nc.sync.dma_start(out=q_raw[i][:, cols], in_=q2[i * P : (i + 1) * P, cols])

        def load_mask(i):
            nc.sync.dma_start(out=mask_sb[i][:], in_=mask[i * P : (i + 1) * P, :])

        def load_vp():
            v_raw[1] = fixed.tile([P, 2, 2, KV * HD], BF16, name="v_raw1")
            for h in range(2):
                nc.sync.dma_start(
                    out=v_raw[1][h * HALF : (h + 1) * HALF], in_=v2[0 : 2 * P, :].rearrange("(u p e) c -> p u e c", u=2, e=2)
                )

        def load_v():
            v_raw[0] = fixed.tile([P, 2, 2, KV * HD], BF16, name="v_raw0")
            nc.sync.dma_start(out=v_raw[0][:], in_=v2.rearrange("(u p e) c -> p u e c", u=2, e=2))

        v_raw = {}
        first, second, third, fourth = TILE_ORDER
        load_mask(first)
        load_k(0, 2)
        load_q(first, 0, GROUP)
        load_q(first, GROUP, GROUP)
        load_k(2, 2)
        load_v()
        load_k(4, 4)
        load_q(first, 2 * GROUP, 2 * GROUP)
        load_wo(0)
        load_wo(1)
        load_mask(second)
        load_q(second, 0, H)
        load_wo(2)
        load_wo(3)
        load_vp()
        for i in (third, fourth):
            load_mask(i)
            load_q(i, 0, H)

        def load_x(i):
            x_rows[i] = fixed.tile([P, D], BF16, name="q_raw%d" % i)
            nc.sync.dma_start(out=x_rows[i][:], in_=x2[i * P : (i + 1) * P, :])


        warm = fixed.tile([P, BANK], BF16)
        nc.vector.memset(warm[:], 0.0)
        make_identity(nc, ident_bf[:])
        make_identity(nc, ident_f32[:])
        nc.gpsimd.memset(vp_half[:], 0)

        def k_job(kv):
            blocks = [k_raw[:, j, kv * HD : (kv + 1) * HD] for j in range(TILES)]
            return (blocks, kT[:, kv, :].rearrange("p (j n) -> p j n", j=TILES), None)

        def q_job(i, g):
            h0 = g * GROUP
            blocks = [q_raw[i][:, (h0 + a) * HD : (h0 + a + 1) * HD] for a in range(GROUP)]
            return (blocks, qT[:, h0 : h0 + GROUP, i * P : (i + 1) * P], None)

        def mask_job(i):
            blocks = [mask_sb[i][:, j * P : (j + 1) * P] for j in range(i + 1)]
            return (blocks, maskT[i][:], ROOT)

        jobs = []
        for r in range(ROUNDS):
            i, g = tile_of_round(r), r % GROUPS
            needed = r * GROUP
            if g == 0 and i in TENSOR_MASK_TILES:
                jobs.append((needed, mask_job(i)))
            if i == first:
                jobs.append((needed, k_job(2 * g)))
            jobs.append((needed, q_job(i, g)))
            if i == first:
                jobs.append((needed + 2, k_job(2 * g + 1)))

        def flip_job(job):
            flip = ps_ring.tile([P, 4, P], BF16, name="ring")
            for c, block in enumerate(job[0]):
                nc.tensor.matmul(flip[:, c, :], lhsT=block, rhs=ident_bf[:], start=True, stop=True)
            return flip

        def finish_job(job, flip, on_scalar):
            blocks, dst, factor = job
            turned = flip[:, 0 : len(blocks), :]
            if factor is None:
                if on_scalar:
                    nc.scalar.copy(out=dst, in_=turned)
                else:
                    nc.vector.tensor_copy(out=dst, in_=turned)
            elif on_scalar:
                nc.scalar.activation(out=dst, in_=turned, func=ACT.Copy, scale=factor)
            else:
                nc.vector.tensor_scalar(out=dst, in0=turned, scalar1=factor, scalar2=None, op0=ALU.mult)

        warm_sums = ps_ring.tile([P, BANK], F32, name="ring")
        for n in range(WARM_MATMULS):
            nc.tensor.matmul(warm_sums[:], lhsT=warm[:, 0:P], rhs=warm[:], start=True, stop=True)

        for n in range(HEAD_JOBS):
            finish_job(jobs[n][1], flip_job(jobs[n][1]), n % 2 == 0)
        latest = []
        limit = STEPS
        for needed, job in reversed(jobs[HEAD_JOBS:]):
            limit = min(limit - (1 if len(jobs) - len(latest) <= HEAD_JOBS + DENSE_JOBS else 2), needed - JOB_LEAD)
            latest.append((limit, job))
        job_at_step = {}
        free = 0
        for limit, job in reversed(latest):
            free = max(free, limit)
            job_at_step[free] = job
            free += 1
        x_at_step = {}
        for n, i in enumerate(TILE_ORDER):
            x_step = max(X_STEP + n * GROUP, (n + 1) * GROUPS * GROUP - GROUP - JOB_LEAD + X_LAG)
            x_at_step.setdefault(x_step, []).append(i)

        banks = []
        bank_at_step = {}
        for r in range(ROUNDS):
            i = tile_of_round(r)
            per_bank = BANK // keys_of(i)
            for a in range(0, GROUP, per_bank):
                bank_at_step[r * GROUP + a] = len(banks)
                banks.append((i, (r % GROUPS) * GROUP + a, per_bank, r < VECTOR_MASK_ROUND))
        score_tiles = {}
        head_scores = {}

        def issue_scores(b):
            i, h0, per_bank, on_tensor = banks[b]
            keys = keys_of(i)
            if b == BORROWED:
                scores = ps_ring.tile([P, BANK], F32, name="ring")
            else:
                scores = ps_scores.tile([P, BANK], F32, name="scores")
            for a in range(per_bank):
                for j in range(i + 1 if on_tensor else 0):
                    nc.tensor.matmul(
                        scores[:, a * keys + j * P : a * keys + (j + 1) * P],
                        lhsT=maskT[i][:, j, :],
                        rhs=ident_f32[:],
                        start=(a == 0 and j == 0),
                        stop=False,
                        is_transpose=True,
                    )
            for a in range(per_bank):
                nc.tensor.matmul(
                    scores[:, a * keys : (a + 1) * keys],
                    lhsT=qT[:, h0 + a, i * P : (i + 1) * P],
                    rhs=kT[:, (h0 + a) // 2, 0:keys],
                    start=(not on_tensor),
                    stop=(not on_tensor or a == per_bank - 1),
                )
            score_tiles[b] = scores

        def add_mask(step):
            b = bank_at_step[step]
            i, h0, per_bank, on_tensor = banks[b]
            keys = keys_of(i)
            masked = work.tile([P, BANK], F32, name="masked", bufs=3)
            nc.vector.scalar_tensor_tensor(
                out=masked[:, 0 : per_bank * keys].rearrange("p (a n) -> p a n", a=per_bank),
                in0=score_tiles[b][:, 0 : per_bank * keys].rearrange("p (a n) -> p a n", a=per_bank),
                scalar=SCALE,
                in1=mask_sb[i][:, 0:keys].unsqueeze(1).to_broadcast([P, per_bank, keys]),
                op0=ALU.mult,
                op1=ALU.add,
            )
            score_tiles[b] = masked

        def row_max(step):
            b = bank_at_step[step]
            i, h0, per_bank, on_tensor = banks[b]
            keys = keys_of(i)
            cols = slice(step, step + per_bank)
            nc.vector.tensor_reduce(
                out=(rawmax if on_tensor else negmax)[:, cols],
                in_=score_tiles[b][:, 0 : per_bank * keys].rearrange("p (a n) -> p a n", a=per_bank),
                axis=mybir.AxisListType.X,
                op=ALU.max,
                negate=True,
            )
            for a in range(per_bank):
                head_scores[step + a] = score_tiles[b][:, a * keys : (a + 1) * keys]

        def scale_max(step):
            cols = slice(step, step + banks[bank_at_step[step]][2])
            nc.scalar.activation(out=scaledmax[:, cols], in_=rawmax[:, cols], func=ACT.Copy, scale=SCALE)

        def exponentials(step):
            i = tile_of_round(step // GROUP)
            on_tensor = step // GROUP < VECTOR_MASK_ROUND
            keys = keys_of(i)
            if i in PAIRED:
                n = step // 2 % E_TILES
                used = i + 1
                dst = e_tiles[n][:].rearrange("p (u h k) -> p h u k", u=2, h=2)[:, step % 2, 0:used, :]
                src = head_scores[step].rearrange("p (u k) -> p u k", k=P)
                filled = 2 * keys
            else:
                n = step % E_TILES
                dst = e_tiles[n][:, 0:keys]
                src = head_scores[step]
                filled = keys
            if filled < e_filled[n]:
                nc.gpsimd.memset(e_tiles[n][:, filled : e_filled[n]], 0.0)
            e_filled[n] = filled
            nc.scalar.activation(
                out=dst,
                in_=src,
                func=ACT.Exp,
                bias=(scaledmax if on_tensor else negmax)[:, step : step + 1],
                scale=SCALE if on_tensor else 1.0,
                accum_out=rowsum[:, step : step + 1],
            )

        e_flips = {}
        e_grouped = {}
        e_codes = {}
        e_scales = {}
        head_sums = {}
        o_rows = {}
        o_flips = {}
        o_grouped = {}

        def flip_e(r, half):
            paired = tile_of_round(r) in PAIRED
            flip = ps_ring.tile([P, 4, P], F32, name="ring")
            for a in range(2):
                n = 2 * r + a if paired else r * GROUP + 2 * half + a
                words = e_tiles[n % E_TILES][:].bitcast(F32)
                for u in range(2):
                    nc.tensor.transpose(flip[:, 2 * a + u, :], words[:, u * P : (u + 1) * P], ident_f32[:])
            e_flips[(r, half)] = flip

        def gather_e(r, half):
            paired = tile_of_round(r) in PAIRED
            if r not in e_grouped:
                e_grouped[r] = work.tile([P, GROUP * P * 4], BF16, name="e_grouped", align_bytes=64)
            e_words = e_grouped[r][:].bitcast(F32).rearrange("p (a q u) -> p a q u", a=GROUP, u=2)
            a0 = 0 if paired else 2 * half
            nc.scalar.copy(
                out=e_words[:, a0 : a0 + 2], in_=e_flips[(r, half)][:].rearrange("p (a u) q -> p a q u", u=2)
            )

        def quantise_e(r):
            columns = P * (GROUP // 2 if tile_of_round(r) in PAIRED else GROUP)
            e_codes[r] = work.tile([P, GROUP * P], U32, name="e_codes", align_bytes=64)
            e_scales[r] = work.tile([P, GROUP * P], U8, name="e_scales", align_bytes=64)
            nc.vector.quantize_mx(
                out=e_codes[r][:, 0:columns].bitcast(FP8X4),
                scales=e_scales[r][:, 0:columns],
                in_=e_grouped[r][:, 0 : 4 * columns],
            )
            c0 = r * GROUP
            nc.vector.reciprocal(out=rinv[:, c0 : c0 + GROUP], in_=rowsum[:, c0 : c0 + GROUP])

        def heads_matmul(r):
            paired = tile_of_round(r) in PAIRED
            head_sums[r] = ps_ring.tile([P, GROUP, HD], F32, name="ring")
            for a in range(GROUP):
                kv = ((r % GROUPS) * GROUP + a) // 2
                queries = slice((a // 2 if paired else a) * P, (a // 2 + 1 if paired else a + 1) * P)
                features = slice(kv * HD, (kv + 1) * HD)
                codes, scales = (vp_half[:, a % 2, :], vp_scales) if paired else (v_codes[:], v_scales)
                nc.tensor.matmul_mx(
                    out=head_sums[r][:, a, :],
                    lhsT=e_codes[r][:, queries].bitcast(FP8X4),
                    lhsT_scale=e_scales[r][:, queries],
                    rhs=codes[:, features].bitcast(FP8X4),
                    rhs_scale=scales[:, features],
                    start=True,
                    stop=True,
                )

        def normalise(r):
            o_rows[r] = work.tile([P, GROUP * HD], BF16, name="o_rows")
            for a in range(GROUP):
                nc.scalar.activation(
                    out=o_rows[r][:, a * HD : (a + 1) * HD],
                    in_=head_sums[r][:, a, :],
                    func=ACT.Copy,
                    scale=rinv[:, r * GROUP + a : r * GROUP + a + 1],
                )

        def flip_o(r):
            o_flips[r] = ps_ring.tile([P, 4, P], F32, name="ring")
            words = o_rows[r][:].bitcast(F32)
            for u in range(2):
                nc.tensor.transpose(o_flips[r][:, u, :], words[:, u * P : (u + 1) * P], ident_f32[:])

        def gather_o(r):
            o_grouped[r] = work.tile([P, P * 4], BF16, name="o_grouped", align_bytes=64)
            nc.scalar.copy(
                out=o_grouped[r][:].bitcast(F32).rearrange("p (q u) -> p q u", u=2),
                in_=o_flips[r][:, 0:2, :].rearrange("p u q -> p q u"),
            )

        def quantise_o(r):
            i = tile_of_round(r)
            g = r % GROUPS
            rows = slice(i * P, (i + 1) * P)
            nc.vector.quantize_mx(
                out=o_codes[:, g, rows].bitcast(FP8X4), scales=o_scales[:, g, rows], in_=o_grouped[r][:]
            )

        v_grouped = {}

        def interleave_v(which, n):
            if n == 0:
                v_grouped[which] = fixed.tile([P, KV * HD, 4], BF16, name="v_grouped", align_bytes=64)
            width = KV * HD // V_PARTS
            part = slice(n * width, (n + 1) * width)
            dst = v_grouped[which][:, part, :].rearrange("p (c i) t -> p c t i", i=4)
            src = v_raw[which][:, :, :, part].rearrange("p u e (c i) -> p c (u e) i", i=4)
            nc.gpsimd.tensor_scalar(out=dst, in0=src, scalar1=1.0, scalar2=0.0, op0=ALU.mult, op1=ALU.add)

        def quantise_v(which, part, parts):
            codes, scales = ((v_codes, v_scales), (vp_codes, vp_scales))[which]
            width = KV * HD // parts
            cols = slice(part * width, (part + 1) * width)
            nc.vector.quantize_mx(
                out=codes[:, cols].bitcast(FP8X4),
                scales=scales[:, cols],
                in_=v_grouped[which][:, cols, :].rearrange("p c t -> p (c t)"),
            )

        def spread_vp():
            for h in range(2):
                rows = slice(h * HALF, (h + 1) * HALF)
                nc.gpsimd.tensor_copy(out=vp_half[rows, h, :], in_=vp_codes[rows, :])

        wo_flips = {}
        wo_grouped = {}

        def flip_wo(item):
            pr, g = divmod(item, GROUPS)
            flip = ps_ring.tile([P, 4, P], F32, name="ring")
            for r in range(2):
                words = wo_raw[pr][:, r, :].bitcast(F32)
                for u in range(2):
                    w0 = 256 * g + 128 * u
                    nc.tensor.transpose(flip[:, 2 * r + u, :], words[:, w0 : w0 + P], ident_f32[:])
            wo_flips[item] = flip

        def gather_wo(item):
            wo_grouped[item] = work.tile([P, 4 * 2 * P], BF16, name="wo_grouped", align_bytes=64, bufs=3)
            dst = wo_grouped[item][:].bitcast(F32).rearrange("p (r d u) -> p r d u", r=2, u=2)
            src = wo_flips[item][:].rearrange("p (r u) d -> p r d u", u=2)
            if item % VECTOR_WO == VECTOR_WO - 1:
                nc.vector.tensor_copy(out=dst, in_=src)
            else:
                nc.scalar.copy(out=dst, in_=src)

        def quantise_wo(item):
            pr, g = divmod(item, GROUPS)
            cols = slice(pr * 2 * P, (pr + 1) * 2 * P)
            nc.vector.quantize_mx(
                out=wo_codes[:, g, cols].bitcast(FP8X4), scales=wo_scales[:, g, cols], in_=wo_grouped[item][:]
            )

        sums = {}

        def project(i, n, groups):
            rows = slice(i * P, (i + 1) * P)
            cols = slice(n * BANK, (n + 1) * BANK)
            if groups[0] == 0:
                if i == TILE_ORDER[-1] and n < SCORE_BANKS:
                    sums[(i, n)] = ps_scores.tile([P, BANK], F32, name="scores")
                else:
                    sums[(i, n)] = ps_ring.tile([P, BANK], F32, name="ring")
            for g in groups:
                nc.tensor.matmul_mx(
                    out=sums[(i, n)][:],
                    lhsT=o_codes[:, g, rows].bitcast(FP8X4),
                    lhsT_scale=o_scales[:, g, rows],
                    rhs=wo_codes[:, g, cols].bitcast(FP8X4),
                    rhs_scale=wo_scales[:, g, cols],
                    start=(g == 0),
                    stop=(g == GROUPS - 1),
                )

        def add_residual(i, n):
            rows = slice(i * P, (i + 1) * P)
            cols = slice(n * BANK, (n + 1) * BANK)
            result = work.tile([P, BANK], F32, name="result", bufs=6)
            nc.vector.tensor_tensor(out=result[:], in0=sums[(i, n)][:], in1=x_rows[i][:, cols], op=ALU.add)
            nc.sync.dma_start(out=out2[rows, cols], in_=result[:])

        project_steps = {}
        residual_steps = {}
        whole = tuple(range(GROUPS))

        def plan(step, i, n, groups):
            project_steps.setdefault(step, []).append((i, n, groups))
            if groups[-1] == GROUPS - 1:
                residual_steps.setdefault(step + 1, []).append((i, n))

        r = 0
        for i in TILE_ORDER[:-1]:
            o_ready = GROUP * ((TILE_ORDER.index(i) + 1) * GROUPS - 1) + O_QUANT
            for n in range(BLOCKS - (KEPT_BACK if i == TILE_ORDER[-2] else 0)):
                wo_ready = WO_STEP + (n + 1) * WO_ITEMS // BLOCKS - 1 + WO_QUANT_LAG
                r = max(r, -(-max(o_ready, wo_ready) // GROUP))
                plan(min(r, ROUNDS + 1) * GROUP + PROJECT, i, n, whole)
                r += 1
        o_done = (ROUNDS - 1) * GROUP + O_QUANT
        for n in range(SCORE_BANKS):
            plan(o_done - BLOCKS + n, TILE_ORDER[-1], n, whole[:-1])
        for n in range(SCORE_BANKS):
            plan(o_done, TILE_ORDER[-1], n, whole[-1:])
        for n in range(BLOCKS - KEPT_BACK, BLOCKS):
            plan(o_done, TILE_ORDER[-2], n, whole)
        for n in range(SCORE_BANKS, BLOCKS):
            plan(o_done, TILE_ORDER[-1], n, whole)
        last_step = max(residual_steps)

        def item_at(step):
            item = step - WO_STEP
            return item if 0 <= item < WO_ITEMS else None

        def rounds_at(step, offset):
            r, a = divmod(step - offset, GROUP)
            return [r] if a == 0 and 0 <= r < ROUNDS else []

        def halves_at(step, offsets):
            pairs = [(r, half) for half in range(2) for r in rounds_at(step, offsets[half])]
            return [(r, half) for r, half in pairs if half == 1 or tile_of_round(r) not in PAIRED]

        issue_at_step = {}
        for first_head, b in bank_at_step.items():
            early = 1 if banks[b][3] else 1 + MASK_LEAD
            issue_at_step.setdefault(first_head - early, []).append(b)
        for b in issue_at_step[-1]:
            issue_scores(b)
        for step in range(last_step + 1):
            item = item_at(step)
            on_tensor = step in bank_at_step and banks[bank_at_step[step]][3]
            ahead = step + MASK_LEAD

            if on_tensor:
                row_max(step)
            if ahead in bank_at_step and not banks[bank_at_step[ahead]][3]:
                add_mask(ahead)
                row_max(ahead)
            for r in rounds_at(step, E_QUANT):
                quantise_e(r)
            for r in rounds_at(step, NORMALISE):
                normalise(r)
            for r in rounds_at(step, O_QUANT):
                quantise_o(r)
            if item_at(step - WO_QUANT_LAG) is not None:
                quantise_wo(item_at(step - WO_QUANT_LAG))
            quarter, phase = divmod(step - V_STEP, GROUP)
            if 0 <= quarter < V_QUARTERS:
                if phase == 0:
                    interleave_v(0, 2 * quarter)
                    interleave_v(0, 2 * quarter + 1)
            if 0 <= step - VP_STEP < V_PARTS:
                interleave_v(1, step - VP_STEP)
            elif step == VP_STEP + V_PARTS:
                quantise_v(1, 0, 1)
            elif step == VP_STEP + V_PARTS + 2:
                spread_vp()

            if step in job_at_step:
                job_flip = flip_job(job_at_step[step])
            if item is not None:
                flip_wo(item)
                if item % GROUPS == GROUPS - 1 and item // GROUPS + WO_BUFS < WO_PAIRS:
                    load_wo(item // GROUPS + WO_BUFS)
            for b in issue_at_step.get(step, ()):
                if banks[b][3]:
                    issue_scores(b)
            if 0 <= step - 1 < STEPS:
                exponentials(step - 1)
            for r, half in halves_at(step, E_FLIP):
                flip_e(r, half)
            for r, half in halves_at(step, E_GATHER):
                gather_e(r, half)
            for r in rounds_at(step, HEADS):
                heads_matmul(r)
            for r in rounds_at(step, O_FLIP):
                flip_o(r)
            for block in project_steps.get(step, ()):
                project(*block)

            for b in issue_at_step.get(step, ()):
                if not banks[b][3]:
                    issue_scores(b)

            if 0 <= quarter < V_QUARTERS and phase == 1:
                quantise_v(0, quarter, V_QUARTERS)
            if on_tensor:
                scale_max(step)
            for r in rounds_at(step, O_GATHER):
                gather_o(r)
            if step in job_at_step:
                finish_job(job_at_step[step], job_flip, False)
            if item is not None:
                gather_wo(item)
            for block in residual_steps.get(step, ()):
                add_residual(*block)
            for i in x_at_step.get(step, ()):
                load_x(i)
